import numpy as np
import ml_dtypes


def mxq(x, axis, fmt="e4m3"):
    dtype, down = {"e4m3": (ml_dtypes.float8_e4m3fn, 7), "e5m2": (ml_dtypes.float8_e5m2, 14)}[fmt]
    v = np.moveaxis(np.asarray(x, np.float32).astype(ml_dtypes.bfloat16).astype(np.float64), axis, -1)
    blocks = v.reshape(v.shape[:-1] + (-1, 32))
    amax = np.abs(blocks).max(-1, keepdims=True)
    byte = np.maximum(np.where(amax > 0, np.frexp(amax)[1] - 1 + 127, 0) - down, 1)
    scale = np.exp2(byte - 127.0)
    codes = (blocks / scale).astype(np.float32).astype(dtype).astype(np.float64)
    return np.moveaxis((codes * scale).reshape(v.shape), -1, axis)


WIDE = False


def mx_kscale(k):
    if not WIDE:
        return np.ones(k)
    levels = np.array([10, -10, 5, -5, 0])
    a = np.random.permutation(np.resize(levels, k // 512 * 4)).reshape(k // 512, 4)
    idx = np.arange(k)
    return np.exp2(a[idx // 512, idx % 128 // 32])


BF16 = ml_dtypes.bfloat16


def bf(x):
    return np.asarray(x, np.float32).astype(BF16)


def f64(x):
    return np.asarray(x).astype(np.float64)


E2M1 = np.array([0.0, 0.5, 1.0, 1.5, 2.0, 3.0, 4.0, 6.0, -0.0, -0.5, -1.0, -1.5, -2.0, -3.0, -4.0, -6.0])


def pack_weight(w, fmt):
    k, n = w.shape
    w = f64(bf(w)).reshape(k // 32, 32, n)
    amax = np.abs(w).max(1)
    if fmt == "e4m3":
        byte = np.frexp(amax)[1] - 1 + 127 - 7
    else:
        mant, ex = np.frexp(amax / 6.0)
        byte = np.where(mant > 0.5, ex, ex - 1) + 127
    byte = np.clip(np.where(amax > 0, byte, 1), 1, 254)
    scaled = (w * np.exp2(127.0 - byte)[:, None, :]).reshape(k, n).astype(np.float32)
    by_word = np.ascontiguousarray(scaled.reshape(k // 512, 128, 4, n).transpose(0, 1, 3, 2))
    if fmt == "e4m3":
        words = by_word.astype(ml_dtypes.float8_e4m3fn).view(np.uint8)
    else:
        c = by_word.astype(ml_dtypes.float4_e2m1fn).view(np.uint8) & 0xF
        words = c[..., 0::2] | (c[..., 1::2] << 4)
    return np.ascontiguousarray(words), np.ascontiguousarray(byte.astype(np.uint8).reshape(k // 512, 16, n))


def unpack_weight(words, scales, fmt):
    g, p, n, _ = words.shape
    if fmt == "e4m3":
        vals = np.ascontiguousarray(words).view(ml_dtypes.float8_e4m3fn).astype(np.float64)
    else:
        nib = np.empty((g, p, n, 4), np.uint8)
        nib[..., 0::2] = words & 0xF
        nib[..., 1::2] = words >> 4
        vals = E2M1[nib]
    vals = vals * np.repeat(np.exp2(scales.astype(np.float64) - 127.0), 8, axis=1)[..., None]
    return vals.transpose(0, 1, 3, 2).reshape(g * 512, n)


B, H, W, C, D, P = 128, 1, 1, 2048, 3072, 1024
F = H * W * D
STRIDE = 16.0
FMT = "e4m3"


def safe_exp(v):
    return np.exp(np.clip(v, -10.0, 10.0))


def setup_inputs():
    s = mx_kscale(C)
    t = mx_kscale(F)[:D]
    tf = np.tile(t, H * W)[:, None]
    features = bf(np.random.standard_normal((B, H, W, C)) * s)
    roi = bf(np.random.uniform(0.02, 0.125, (B, P, 4)))
    conv_w_words, conv_w_scales = pack_weight(np.random.standard_normal((C, D)) / np.sqrt(C) / s[:, None] * t, FMT)
    conv_b = bf(np.random.standard_normal(D) * 0.2 * t)
    cls_w_words, cls_w_scales = pack_weight(np.random.standard_normal((F, 2 * P)) * 1.5 / np.sqrt(F) / tf, FMT)
    cls_b = bf(np.random.standard_normal(2 * P) * 0.5)
    bbox_w_words, bbox_w_scales = pack_weight(np.random.standard_normal((F, 4 * P)) * 0.7 / np.sqrt(F) / tf, FMT)
    bbox_b = bf(np.random.standard_normal(4 * P) * 0.3)
    return {"features": features,
            "roi": roi,
            "conv_w_words": conv_w_words,
            "conv_w_scales": conv_w_scales,
            "conv_b": conv_b,
            "cls_w_words": cls_w_words,
            "cls_w_scales": cls_w_scales,
            "cls_b": cls_b,
            "bbox_w_words": bbox_w_words,
            "bbox_w_scales": bbox_w_scales,
            "bbox_b": bbox_b}


def reference(features, roi, conv_w_words, conv_w_scales, conv_b, cls_w_words, cls_w_scales, cls_b, bbox_w_words, bbox_w_scales, bbox_b):
    h = np.maximum((mxq(f64(features).reshape(B * H * W, C), 1, "e4m3") @ unpack_weight(conv_w_words, conv_w_scales, FMT)) + f64(conv_b), 0.0)
    flatq = mxq(h.reshape(B, F), 1, "e4m3")
    cls = (flatq @ unpack_weight(cls_w_words, cls_w_scales, FMT)) + f64(cls_b)
    bbox = (flatq @ unpack_weight(bbox_w_words, bbox_w_scales, FMT)[:, P:]) + f64(bbox_b)[P:]
    obj = np.stack([cls[:, :P], cls[:, P:]], axis=0)
    e = np.exp(obj - obj.max(axis=0, keepdims=True))
    objectness = (e / e.sum(axis=0, keepdims=True))[1]
    roi_img = f64(roi) * STRIDE
    bb = np.transpose(bbox.reshape(B, 3, P), (0, 2, 1))
    x = roi_img[:, :, 0] - bb[:, :, 0] * roi_img[:, :, 3]
    y = roi_img[:, :, 1]
    w = roi_img[:, :, 2] * safe_exp(bb[:, :, 1])
    hh = roi_img[:, :, 3] * safe_exp(bb[:, :, 2])
    return np.stack([x, y, w, hh, objectness], axis=-1)

@@ -1,0 +1,270 @@
+from contextlib import ExitStack
+
+import concourse.mybir as mybir
+from concourse.masks import make_identity
+
+F32 = mybir.dt.float32
+BF16 = mybir.dt.bfloat16
+I32 = mybir.dt.int32
+U32 = mybir.dt.uint32
+U8 = mybir.dt.uint8
+FP8X4 = mybir.dt.float8_e4m3fn_x4
+ALU = mybir.AluOpType
+ACT = mybir.ActivationFunctionType
+
+P = 128
+B = 128
+C = 2048
+D = 3072
+NP = 1024
+GC = C // 512
+GD = D // 512
+BANK = 512
+CH = 256
+NCH = NP // CH
+PRE = 1
+N8 = 10
+
+FLOPS = 2 * B * (C * D + D * 2 * NP + D * 3 * NP)
+BYTES = (B * C * 2 + B * NP * 4 * 2 + C * D + C * D // 32 + D * 2 + D * 2 * NP + D * 2 * NP // 32 + 2 * NP * 2
+         + D * 3 * NP + D * 3 * NP // 32 + 3 * NP * 2 + B * NP * 5 * 4)
+
+
+def tile_classifiermodel_w_kernel(tc, features, roi, conv_w_words, conv_w_scales, conv_b,
+                                             cls_w_words, cls_w_scales, cls_b,
+                                             bbox_w_words, bbox_w_scales, bbox_b, out):
+    nc = tc.nc
+
+    def words(ap):
+        return ap.rearrange("p n t -> p (n t)").bitcast(I32)
+
+    with ExitStack() as ctx:
+        const = ctx.enter_context(tc.tile_pool(name="const", bufs=1))
+        wpool = ctx.enter_context(tc.tile_pool(name="weights", bufs=1))
+        psum = ctx.enter_context(tc.psum_pool(name="psum", bufs=8))
+
+        brow = const.tile([P, BANK], BF16)
+        nc.vector.memset(brow[:], 0.0)
+        conv_pl = const.tile([P, D], U8, align_bytes=64)
+        bbox_pl = const.tile([P, 3 * NP], U8, align_bytes=64)
+        cls_pl = const.tile([P, 2 * NP], U8, align_bytes=64)
+        mix_pl = const.tile([P, 3 * NP], U8, align_bytes=64)
+        for pl in (conv_pl, bbox_pl, cls_pl, mix_pl):
+            nc.vector.memset(pl[:].bitcast(I32), 0)
+        ident_f = const.tile([P, P], F32)
+        make_identity(nc, ident_f[:])
+        ident_b = const.tile([P, P], BF16)
+        make_identity(nc, ident_b[:])
+        sel = const.tile([P, 2], BF16)
+        nc.vector.tensor_tensor(out=sel[:], in0=ident_b[:, 14:16], in1=ident_b[:, 12:14], op=ALU.subtract)
+
+        fcodes = const.tile([P, GC * B], U32, align_bytes=64)
+        fscales = const.tile([P, GC * B], U8, align_bytes=64)
+        hcodes = const.tile([P, GD * B], U32, align_bytes=64)
+        hscales = const.tile([P, GD * B], U8, align_bytes=64)
+        bbias = const.tile([P, 3 * NP], BF16)
+        dbias = const.tile([P, NP], F32)
+        roi_sb = const.tile([P, NP, 4], BF16)
+
+        def bbox_scale(g, c0, n):
+            if g < 4:
+                return bbox_pl[4 * g:P, c0:c0 + n]
+            return mix_pl[8 + 4 * (g - 4):P, c0:c0 + n]
+
+        def cls_scale(g, c0, n):
+            if g < 4:
+                return cls_pl[4 * g:P, c0:c0 + n]
+            return mix_pl[4 * (g - 4):P, c0:c0 + n]
+
+        with tc.tile_pool(name="s1", bufs=1) as s1:
+            x_sb = s1.tile([P, C], BF16)
+            nc.sync.dma_start(out=x_sb[:], in_=features.rearrange("b h w c -> b (h w c)"))
+            nc.scalar.dma_start(out=brow[0:6, :], in_=conv_b.rearrange("(r c) -> r c", c=BANK))
+            nc.scalar.dma_start(out=brow[6:12, :], in_=bbox_b[NP:4 * NP].rearrange("(r c) -> r c", c=BANK))
+            nc.scalar.dma_start(out=brow[12:16, :], in_=cls_b.rearrange("(r c) -> r c", c=BANK))
+            nc.sync.dma_start(out=roi_sb[:], in_=roi)
+            for q in range(4):
+                nc.sync.dma_start(out=conv_pl[32 * q:32 * q + 16, :].bitcast(I32),
+                                  in_=conv_w_scales[:, 4 * q:4 * q + 4, :].bitcast(I32))
+            for q in range(4):
+                nc.sync.dma_start(out=bbox_pl[32 * q:32 * q + 16, :].bitcast(I32),
+                                  in_=bbox_w_scales[0:4, 4 * q:4 * q + 4, NP:4 * NP].bitcast(I32))
+            for q in range(4):
+                nc.sync.dma_start(out=mix_pl[32 * q + 8:32 * q + 16, :].bitcast(I32),
+                                  in_=bbox_w_scales[4:6, 4 * q:4 * q + 4, NP:4 * NP].bitcast(I32))
+            for q in range(4):
+                nc.sync.dma_start(out=cls_pl[32 * q:32 * q + 16, :].bitcast(I32),
+                                  in_=cls_w_scales[0:4, 4 * q:4 * q + 4, :].bitcast(I32))
+            for q in range(4):
+                nc.sync.dma_start(out=mix_pl[32 * q:32 * q + 8, 0:2 * NP].bitcast(I32),
+                                  in_=cls_w_scales[4:6, 4 * q:4 * q + 4, :].bitcast(I32))
+            conv_w = []
+            for g in range(GC):
+                w = wpool.tile([P, D], U32, tag="w12", bufs=4, name="convw%d" % g, align_bytes=64)
+                nc.sync.dma_start(out=w[:].bitcast(I32), in_=words(conv_w_words[g]))
+                conv_w.append(w)
+            b23_w = []
+            for g in range(GD):
+                w = wpool.tile([P, 2 * NP], U32, tag="w8", bufs=N8, name="b23w%d" % g, align_bytes=64)
+                nc.sync.dma_start(out=w[:].bitcast(I32), in_=words(bbox_w_words[g][:, 2 * NP:4 * NP, :]))
+                b23_w.append(w)
+
+            x32 = x_sb[:].bitcast(F32)
+            fgrouped = s1.tile([P, C], BF16, align_bytes=64)
+            fg32 = fgrouped[:].bitcast(F32).rearrange("p (g b u) -> p g b u", g=GC, u=2)
+            for a in range(GC // 2):
+                xt = psum.tile([P, 2, 2, B], F32, tag="bank", name="xt%d" % a)
+                for gg in range(2):
+                    g = 2 * a + gg
+                    for u in range(2):
+                        nc.tensor.transpose(xt[:, gg, u, :], x32[:, 256 * g + u:256 * (g + 1):2], ident_f[:])
+                nc.vector.tensor_copy(out=fg32[:, 2 * a:2 * a + 2, :, :], in_=xt[:].rearrange("p g u b -> p g b u"))
+            nc.vector.quantize_mx(out=fcodes[:].bitcast(FP8X4), scales=fscales[:], in_=fgrouped[:])
+
+            cbias = s1.tile([P, D], BF16)
+            for r in range(14):
+                bp = psum.tile([P, BANK], F32, tag="bank", name="bp%d" % r)
+                if r < 12:
+                    lhsT = ident_b[:, r:r + 1].to_broadcast([P, P])
+                else:
+                    lhsT = sel[:, r - 12:r - 11].to_broadcast([P, P])
+                nc.tensor.matmul(out=bp[:], lhsT=lhsT, rhs=brow[:], start=True, stop=True)
+                if r < 6:
+                    dst = cbias[:, BANK * r:BANK * (r + 1)]
+                elif r < 12:
+                    dst = bbias[:, BANK * (r - 6):BANK * (r - 5)]
+                else:
+                    dst = dbias[:, BANK * (r - 12):BANK * (r - 11)]
+                if r % 2 == 0:
+                    nc.vector.tensor_copy(out=dst, in_=bp[:])
+                else:
+                    nc.scalar.copy(out=dst, in_=bp[:])
+
+            hacc = []
+            for j in range(GD):
+                acc = psum.tile([P, BANK], F32, tag="bank", name="hacc%d" % j)
+                hacc.append(acc)
+            for g in range(GC):
+                for j in range(GD):
+                    nc.tensor.matmul_mx(out=hacc[j][:],
+                                        lhsT=fcodes[:, B * g:B * (g + 1)].bitcast(FP8X4),
+                                        lhsT_scale=fscales[:, B * g:B * (g + 1)],
+                                        rhs=conv_w[g][:, BANK * j:BANK * (j + 1)].bitcast(FP8X4),
+                                        rhs_scale=conv_pl[4 * g:P, BANK * j:BANK * (j + 1)],
+                                        start=(g == 0), stop=(g == GC - 1))
+            for j in range(GD):
+                tmp = s1.tile([P, BANK], F32, tag="tmp", bufs=3, name="tmp%d" % j)
+                nc.vector.tensor_tensor(out=tmp[:], in0=hacc[j][:], in1=cbias[:, BANK * j:BANK * (j + 1)], op=ALU.add)
+                hperm = s1.tile([P, 4, P], BF16, tag="hperm", bufs=3, name="hperm%d" % j)
+                nc.scalar.activation(out=hperm[:], in_=tmp[:].rearrange("p (q t) -> p t q", t=4), func=ACT.Relu)
+                ht = psum.tile([P, 4, B], BF16, tag="bank", name="ht%d" % j)
+                for t in range(4):
+                    nc.tensor.transpose(ht[:, t, :], hperm[:, t, :], ident_b[:])
+                hg = s1.tile([P, B, 4], BF16, tag="hg", bufs=3, name="hg%d" % j, align_bytes=64)
+                if j % 2 == 0:
+                    nc.vector.tensor_copy(out=hg[:], in_=ht[:].rearrange("p t b -> p b t"))
+                else:
+                    nc.scalar.copy(out=hg[:], in_=ht[:].rearrange("p t b -> p b t"))
+                nc.vector.quantize_mx(out=hcodes[:, B * j:B * (j + 1)].bitcast(FP8X4),
+                                      scales=hscales[:, B * j:B * (j + 1)],
+                                      in_=hg[:].rearrange("p b t -> p (b t)"))
+
+        def head_pass(acc, g, rhs, rhs_scale):
+            nc.tensor.matmul_mx(out=acc,
+                                lhsT=hcodes[:, B * g:B * (g + 1)].bitcast(FP8X4),
+                                lhsT_scale=hscales[:, B * g:B * (g + 1)],
+                                rhs=rhs.bitcast(FP8X4), rhs_scale=rhs_scale,
+                                start=(g == 0), stop=(g == GD - 1))
+
+        with tc.tile_pool(name="s2", bufs=1) as s2:
+            planes = s2.tile([P, 5, NP], F32)
+            nc.scalar.activation(out=planes[:, 1, :], in_=roi_sb[:, :, 1], func=ACT.Copy, scale=16.0)
+            for hf in range(2):
+                sl = slice(BANK * hf, BANK * (hf + 1))
+                m = s2.tile([P, BANK], F32, tag="u", bufs=3, name="m%d" % hf)
+                nc.vector.scalar_tensor_tensor(out=m[:], in0=bbias[:, sl], scalar=16.0, in1=roi_sb[:, sl, 3],
+                                               op0=ALU.mult, op1=ALU.mult)
+                nc.vector.scalar_tensor_tensor(out=planes[:, 0, sl], in0=roi_sb[:, sl, 0], scalar=16.0, in1=m[:],
+                                               op0=ALU.mult, op1=ALU.subtract)
+
+            b23acc = []
+            for j in range(4):
+                acc = psum.tile([P, BANK], F32, tag="bank", name="b23acc%d" % j)
+                b23acc.append(acc)
+            for g in range(GD):
+                for j in range(4):
+                    head_pass(b23acc[j][:], g, b23_w[g][:, BANK * j:BANK * (j + 1)],
+                              bbox_scale(g, NP + BANK * j, BANK))
+
+            b1_w = []
+            cls_w = []
+
+            def load_b1(c):
+                w = wpool.tile([P, GD, CH], U32, tag="w12", bufs=4, name="b1w%d" % c, align_bytes=64)
+                nc.sync.dma_start(out=w[:].bitcast(I32),
+                                  in_=bbox_w_words[:, :, NP + CH * c:NP + CH * (c + 1), :]
+                                  .rearrange("g p n t -> p g (n t)").bitcast(I32))
+                b1_w.append(w)
+
+            for c in range(PRE):
+                load_b1(c)
+            for g in range(GD):
+                w = wpool.tile([P, 2 * NP], U32, tag="w8", bufs=N8, name="clsw%d" % g, align_bytes=64)
+                nc.sync.dma_start(out=w[:].bitcast(I32), in_=words(cls_w_words[g]))
+                cls_w.append(w)
+            for c in range(PRE, NCH):
+                load_b1(c)
+
+            e = None
+            for j in range(4):
+                comp = 2 + j // 2
+                sl = slice(BANK * (j % 2), BANK * (j % 2 + 1))
+                u = s2.tile([P, BANK], F32, tag="u", bufs=3, name="u%d" % j)
+                nc.vector.tensor_tensor(out=u[:], in0=b23acc[j][:], in1=bbias[:, NP + BANK * j:NP + BANK * (j + 1)],
+                                        op=ALU.add)
+                nc.vector.tensor_scalar(out=u[:], in0=u[:], scalar1=10.0, scalar2=-10.0, op0=ALU.min, op1=ALU.max)
+                e = s2.tile([P, BANK], F32, tag="e", bufs=3, name="e%d" % j)
+                nc.scalar.activation(out=e[:], in_=u[:], func=ACT.Exp)
+                nc.vector.scalar_tensor_tensor(out=planes[:, comp, sl], in0=e[:], scalar=16.0, in1=roi_sb[:, sl, comp],
+                                               op0=ALU.mult, op1=ALU.mult)
+            warm = s2.tile([P, 1], F32)
+            nc.scalar.activation(out=warm[:], in_=e[:, 0:1], func=ACT.Sigmoid)
+
+            def x_chunk(c):
+                sl = slice(CH * c, CH * (c + 1))
+                acc = psum.tile([P, CH], F32, tag="bank", name="b1acc%d" % c)
+                for g in range(GD):
+                    head_pass(acc[:], g, b1_w[c][:, g, :], bbox_scale(g, CH * c, CH))
+                tx = s2.tile([P, CH], F32, tag="tx", bufs=2, name="tx%d" % c)
+                nc.vector.scalar_tensor_tensor(out=tx[:], in0=acc[:], scalar=16.0, in1=roi_sb[:, sl, 3],
+                                               op0=ALU.mult, op1=ALU.mult)
+                nc.vector.tensor_tensor(out=planes[:, 0, sl], in0=planes[:, 0, sl], in1=tx[:], op=ALU.subtract)
+
+            for c in range(PRE):
+                x_chunk(c)
+
+            clsacc = []
+            for j in range(4):
+                acc = psum.tile([P, BANK], F32, tag="bank", name="clsacc%d" % j)
+                clsacc.append(acc)
+            order = (2, 0, 3, 1)
+            for g in range(GD):
+                for j in order:
+                    head_pass(clsacc[j][:], g, cls_w[g][:, BANK * j:BANK * (j + 1)], cls_scale(g, BANK * j, BANK))
+            for hf in range(2):
+                sl = slice(BANK * hf, BANK * (hf + 1))
+                d = s2.tile([P, BANK], F32, tag="d", bufs=2, name="d%d" % hf)
+                nc.vector.tensor_tensor(out=d[:], in0=clsacc[2 + hf][:], in1=dbias[:, sl], op=ALU.add)
+                nc.vector.tensor_tensor(out=d[:], in0=d[:], in1=clsacc[hf][:], op=ALU.subtract)
+                nc.scalar.activation(out=planes[:, 4, sl], in_=d[:], func=ACT.Sigmoid)
+
+            for c in range(NCH):
+                if c >= PRE:
+                    x_chunk(c)
+                sl = slice(CH * c, CH * (c + 1))
+                ob = s2.tile([P, CH, 5], F32, tag="ob", bufs=4, name="ob%d" % c)
+                if c % 2 == 0:
+                    nc.vector.tensor_copy(out=ob[:], in_=planes[:, :, sl].rearrange("p c n -> p n c"))
+                else:
+                    nc.scalar.copy(out=ob[:], in_=planes[:, :, sl].rearrange("p c n -> p n c"))
+                nc.sync.dma_start(out=out[:, sl, :], in_=ob[:])

@@ -87,17 +87,17 @@ def tile_classifiermodel_w_kernel(tc, features, roi, conv_w_words, conv_w_scales
                 nc.sync.dma_start(out=conv_pl[32 * q:32 * q + 16, :].bitcast(I32),
                                   in_=conv_w_scales[:, 4 * q:4 * q + 4, :].bitcast(I32))
             for q in range(4):
-                nc.sync.dma_start(out=bbox_pl[32 * q:32 * q + 16, :].bitcast(I32),
-                                  in_=bbox_w_scales[0:4, 4 * q:4 * q + 4, NP:4 * NP].bitcast(I32))
+                nc.gpsimd.dma_start(out=bbox_pl[32 * q:32 * q + 16, :].bitcast(F32),
+                                  in_=bbox_w_scales[0:4, 4 * q:4 * q + 4, NP:4 * NP].bitcast(F32))
             for q in range(4):
-                nc.sync.dma_start(out=mix_pl[32 * q + 8:32 * q + 16, :].bitcast(I32),
-                                  in_=bbox_w_scales[4:6, 4 * q:4 * q + 4, NP:4 * NP].bitcast(I32))
+                nc.gpsimd.dma_start(out=mix_pl[32 * q + 8:32 * q + 16, :].bitcast(F32),
+                                  in_=bbox_w_scales[4:6, 4 * q:4 * q + 4, NP:4 * NP].bitcast(F32))
             for q in range(4):
-                nc.sync.dma_start(out=cls_pl[32 * q:32 * q + 16, :].bitcast(I32),
-                                  in_=cls_w_scales[0:4, 4 * q:4 * q + 4, :].bitcast(I32))
+                nc.gpsimd.dma_start(out=cls_pl[32 * q:32 * q + 16, :].bitcast(F32),
+                                  in_=cls_w_scales[0:4, 4 * q:4 * q + 4, :].bitcast(F32))
             for q in range(4):
-                nc.sync.dma_start(out=mix_pl[32 * q:32 * q + 8, 0:2 * NP].bitcast(I32),
-                                  in_=cls_w_scales[4:6, 4 * q:4 * q + 4, :].bitcast(I32))
+                nc.gpsimd.dma_start(out=mix_pl[32 * q:32 * q + 8, 0:2 * NP].bitcast(F32),
+                                  in_=cls_w_scales[4:6, 4 * q:4 * q + 4, :].bitcast(F32))
             conv_w = []
             for g in range(GC):
                 w = wpool.tile([P, D], U32, tag="w12", bufs=4, name="convw%d" % g, align_bytes=64)

@@ -20,10 +20,11 @@ NP = 1024
 GC = C // 512
 GD = D // 512
 BANK = 512
-CH = 256
-NCH = NP // CH
+HALF = D // 2
+CHUNKS = ((0, 256), (256, 256), (512, 256), (768, 128), (896, 128))
 PRE = 1
-N8 = 10
+COPY_ON_SCALAR = (2,)
+N8 = 8
 
 FLOPS = 2 * B * (C * D + D * 2 * NP + D * 3 * NP)
 BYTES = (B * C * 2 + B * NP * 4 * 2 + C * D + C * D // 32 + D * 2 + D * 2 * NP + D * 2 * NP // 32 + 2 * NP * 2
@@ -49,7 +50,7 @@ def tile_classifiermodel_w_kernel(tc, features, roi, conv_w_words, conv_w_scales
         bbox_pl = const.tile([P, 3 * NP], U8, align_bytes=64)
         cls_pl = const.tile([P, 2 * NP], U8, align_bytes=64)
         mix_pl = const.tile([P, 3 * NP], U8, align_bytes=64)
-        for pl in (conv_pl, bbox_pl, cls_pl, mix_pl):
+        for pl in (conv_pl, bbox_pl, mix_pl, cls_pl):
             nc.vector.memset(pl[:].bitcast(I32), 0)
         ident_f = const.tile([P, P], F32)
         make_identity(nc, ident_f[:])
@@ -62,6 +63,8 @@ def tile_classifiermodel_w_kernel(tc, features, roi, conv_w_words, conv_w_scales
         fscales = const.tile([P, GC * B], U8, align_bytes=64)
         hcodes = const.tile([P, GD * B], U32, align_bytes=64)
         hscales = const.tile([P, GD * B], U8, align_bytes=64)
+        ncodes = const.tile([P, GD * B], U32, align_bytes=64)
+        nscales = const.tile([P, GD * B], U8, align_bytes=64)
         bbias = const.tile([P, 3 * NP], BF16)
         dbias = const.tile([P, NP], F32)
         roi_sb = const.tile([P, NP, 4], BF16)
@@ -76,33 +79,47 @@ def tile_classifiermodel_w_kernel(tc, features, roi, conv_w_words, conv_w_scales
                 return cls_pl[4 * g:P, c0:c0 + n]
             return mix_pl[4 * (g - 4):P, c0:c0 + n]
 
+        def spread_bias(r, dst, on_vector):
+            bp = psum.tile([P, BANK], F32, tag="bank", name="bp%d" % r)
+            if r < 12:
+                lhsT = ident_b[:, r:r + 1].to_broadcast([P, P])
+            else:
+                lhsT = sel[:, r - 12:r - 11].to_broadcast([P, P])
+            nc.tensor.matmul(out=bp[:], lhsT=lhsT, rhs=brow[:], start=True, stop=True)
+            if on_vector:
+                nc.vector.tensor_copy(out=dst, in_=bp[:])
+            else:
+                nc.scalar.copy(out=dst, in_=bp[:])
+
         with tc.tile_pool(name="s1", bufs=1) as s1:
             x_sb = s1.tile([P, C], BF16)
             nc.sync.dma_start(out=x_sb[:], in_=features.rearrange("b h w c -> b (h w c)"))
             nc.scalar.dma_start(out=brow[0:6, :], in_=conv_b.rearrange("(r c) -> r c", c=BANK))
             nc.scalar.dma_start(out=brow[6:12, :], in_=bbox_b[NP:4 * NP].rearrange("(r c) -> r c", c=BANK))
             nc.scalar.dma_start(out=brow[12:16, :], in_=cls_b.rearrange("(r c) -> r c", c=BANK))
-            nc.sync.dma_start(out=roi_sb[:], in_=roi)
             for q in range(4):
                 nc.sync.dma_start(out=conv_pl[32 * q:32 * q + 16, :].bitcast(I32),
                                   in_=conv_w_scales[:, 4 * q:4 * q + 4, :].bitcast(I32))
-            for q in range(4):
-                nc.gpsimd.dma_start(out=bbox_pl[32 * q:32 * q + 16, :].bitcast(F32),
-                                  in_=bbox_w_scales[0:4, 4 * q:4 * q + 4, NP:4 * NP].bitcast(F32))
-            for q in range(4):
-                nc.gpsimd.dma_start(out=mix_pl[32 * q + 8:32 * q + 16, :].bitcast(F32),
-                                  in_=bbox_w_scales[4:6, 4 * q:4 * q + 4, NP:4 * NP].bitcast(F32))
-            for q in range(4):
-                nc.gpsimd.dma_start(out=cls_pl[32 * q:32 * q + 16, :].bitcast(F32),
-                                  in_=cls_w_scales[0:4, 4 * q:4 * q + 4, :].bitcast(F32))
-            for q in range(4):
-                nc.gpsimd.dma_start(out=mix_pl[32 * q:32 * q + 8, 0:2 * NP].bitcast(F32),
-                                  in_=cls_w_scales[4:6, 4 * q:4 * q + 4, :].bitcast(F32))
             conv_w = []
-            for g in range(GC):
-                w = wpool.tile([P, D], U32, tag="w12", bufs=4, name="convw%d" % g, align_bytes=64)
-                nc.sync.dma_start(out=w[:].bitcast(I32), in_=words(conv_w_words[g]))
-                conv_w.append(w)
+            for hf in range(2):
+                for g in range(GC):
+                    w = wpool.tile([P, HALF], U32, tag="w6", bufs=8, name="convw%d_%d" % (hf, g), align_bytes=64)
+                    nc.sync.dma_start(out=w[:].bitcast(I32),
+                                      in_=words(conv_w_words[g][:, HALF * hf:HALF * (hf + 1), :]))
+                    conv_w.append(w)
+            nc.sync.dma_start(out=roi_sb[:], in_=roi)
+            for q in range(4):
+                nc.sync.dma_start(out=bbox_pl[32 * q:32 * q + 16, :].bitcast(I32),
+                                  in_=bbox_w_scales[0:4, 4 * q:4 * q + 4, NP:4 * NP].bitcast(I32))
+            for q in range(4):
+                nc.sync.dma_start(out=mix_pl[32 * q + 8:32 * q + 16, :].bitcast(I32),
+                                  in_=bbox_w_scales[4:6, 4 * q:4 * q + 4, NP:4 * NP].bitcast(I32))
+            for q in range(4):
+                nc.sync.dma_start(out=cls_pl[32 * q:32 * q + 16, :].bitcast(I32),
+                                  in_=cls_w_scales[0:4, 4 * q:4 * q + 4, :].bitcast(I32))
+            for q in range(4):
+                nc.sync.dma_start(out=mix_pl[32 * q:32 * q + 8, 0:2 * NP].bitcast(I32),
+                                  in_=cls_w_scales[4:6, 4 * q:4 * q + 4, :].bitcast(I32))
             b23_w = []
             for g in range(GD):
                 w = wpool.tile([P, 2 * NP], U32, tag="w8", bufs=N8, name="b23w%d" % g, align_bytes=64)
@@ -122,59 +139,57 @@ def tile_classifiermodel_w_kernel(tc, features, roi, conv_w_words, conv_w_scales
             nc.vector.quantize_mx(out=fcodes[:].bitcast(FP8X4), scales=fscales[:], in_=fgrouped[:])
 
             cbias = s1.tile([P, D], BF16)
-            for r in range(14):
-                bp = psum.tile([P, BANK], F32, tag="bank", name="bp%d" % r)
-                if r < 12:
-                    lhsT = ident_b[:, r:r + 1].to_broadcast([P, P])
-                else:
-                    lhsT = sel[:, r - 12:r - 11].to_broadcast([P, P])
-                nc.tensor.matmul(out=bp[:], lhsT=lhsT, rhs=brow[:], start=True, stop=True)
-                if r < 6:
-                    dst = cbias[:, BANK * r:BANK * (r + 1)]
-                elif r < 12:
-                    dst = bbias[:, BANK * (r - 6):BANK * (r - 5)]
-                else:
-                    dst = dbias[:, BANK * (r - 12):BANK * (r - 11)]
-                if r % 2 == 0:
-                    nc.vector.tensor_copy(out=dst, in_=bp[:])
-                else:
-                    nc.scalar.copy(out=dst, in_=bp[:])
+            for r in range(6):
+                spread_bias(r, cbias[:, BANK * r:BANK * (r + 1)], r % 2 == 0)
 
-            hacc = []
-            for j in range(GD):
-                acc = psum.tile([P, BANK], F32, tag="bank", name="hacc%d" % j)
-                hacc.append(acc)
-            for g in range(GC):
-                for j in range(GD):
-                    nc.tensor.matmul_mx(out=hacc[j][:],
-                                        lhsT=fcodes[:, B * g:B * (g + 1)].bitcast(FP8X4),
-                                        lhsT_scale=fscales[:, B * g:B * (g + 1)],
-                                        rhs=conv_w[g][:, BANK * j:BANK * (j + 1)].bitcast(FP8X4),
-                                        rhs_scale=conv_pl[4 * g:P, BANK * j:BANK * (j + 1)],
-                                        start=(g == 0), stop=(g == GC - 1))
-            for j in range(GD):
-                tmp = s1.tile([P, BANK], F32, tag="tmp", bufs=3, name="tmp%d" % j)
-                nc.vector.tensor_tensor(out=tmp[:], in0=hacc[j][:], in1=cbias[:, BANK * j:BANK * (j + 1)], op=ALU.add)
-                hperm = s1.tile([P, 4, P], BF16, tag="hperm", bufs=3, name="hperm%d" % j)
-                nc.scalar.activation(out=hperm[:], in_=tmp[:].rearrange("p (q t) -> p t q", t=4), func=ACT.Relu)
-                ht = psum.tile([P, 4, B], BF16, tag="bank", name="ht%d" % j)
-                for t in range(4):
-                    nc.tensor.transpose(ht[:, t, :], hperm[:, t, :], ident_b[:])
-                hg = s1.tile([P, B, 4], BF16, tag="hg", bufs=3, name="hg%d" % j, align_bytes=64)
-                if j % 2 == 0:
+            for hf in range(2):
+                hacc = []
+                for jj in range(3):
+                    acc = psum.tile([P, BANK], F32, tag="bank", name="hacc%d_%d" % (hf, jj))
+                    hacc.append(acc)
+                for g in range(GC):
+                    for jj in range(3):
+                        j = 3 * hf + jj
+                        nc.tensor.matmul_mx(out=hacc[jj][:],
+                                            lhsT=fcodes[:, B * g:B * (g + 1)].bitcast(FP8X4),
+                                            lhsT_scale=fscales[:, B * g:B * (g + 1)],
+                                            rhs=conv_w[GC * hf + g][:, BANK * jj:BANK * (jj + 1)].bitcast(FP8X4),
+                                            rhs_scale=conv_pl[4 * g:P, BANK * j:BANK * (j + 1)],
+                                            start=(g == 0), stop=(g == GC - 1))
+                if hf == 0:
+                    for r in range(6, 12):
+                        spread_bias(r, bbias[:, BANK * (r - 6):BANK * (r - 5)], r % 2 == 0)
+                    for r in range(12, 14):
+                        spread_bias(r, dbias[:, BANK * (r - 12):BANK * (r - 11)], r % 2 == 0)
+                for jj in range(3):
+                    j = 3 * hf + jj
+                    tmp = s1.tile([P, BANK], F32, tag="tmp", bufs=3, name="tmp%d" % j)
+                    nc.vector.tensor_tensor(out=tmp[:], in0=hacc[jj][:], in1=cbias[:, BANK * j:BANK * (j + 1)],
+                                            op=ALU.add)
+                    hperm = s1.tile([P, 4, P], BF16, tag="hperm", bufs=3, name="hperm%d" % j)
+                    nc.scalar.activation(out=hperm[:], in_=tmp[:].rearrange("p (q t) -> p t q", t=4), func=ACT.Relu)
+                    ht = psum.tile([P, 4, B], BF16, tag="bank", name="ht%d" % j)
+                    for t in range(4):
+                        nc.tensor.transpose(ht[:, t, :], hperm[:, t, :], ident_b[:])
+                    hg = s1.tile([P, B, 4], BF16, tag="hg", bufs=3, name="hg%d" % j, align_bytes=64)
                     nc.vector.tensor_copy(out=hg[:], in_=ht[:].rearrange("p t b -> p b t"))
-                else:
-                    nc.scalar.copy(out=hg[:], in_=ht[:].rearrange("p t b -> p b t"))
-                nc.vector.quantize_mx(out=hcodes[:, B * j:B * (j + 1)].bitcast(FP8X4),
-                                      scales=hscales[:, B * j:B * (j + 1)],
-                                      in_=hg[:].rearrange("p b t -> p (b t)"))
+                    hgn = s1.tile([P, B, 4], BF16, tag="hgn", bufs=3, name="hgn%d" % j, align_bytes=64)
+                    nc.scalar.activation(out=hgn[:], in_=ht[:].rearrange("p t b -> p b t"), func=ACT.Copy, scale=-1.0)
+                    nc.vector.quantize_mx(out=hcodes[:, B * j:B * (j + 1)].bitcast(FP8X4),
+                                          scales=hscales[:, B * j:B * (j + 1)],
+                                          in_=hg[:].rearrange("p b t -> p (b t)"))
+                    nc.vector.quantize_mx(out=ncodes[:, B * j:B * (j + 1)].bitcast(FP8X4),
+                                          scales=nscales[:, B * j:B * (j + 1)],
+                                          in_=hgn[:].rearrange("p b t -> p (b t)"))
 
-        def head_pass(acc, g, rhs, rhs_scale):
+        def head_pass(acc, g, rhs, rhs_scale, start, stop, negated=False):
+            codes = ncodes if negated else hcodes
+            scales = nscales if negated else hscales
             nc.tensor.matmul_mx(out=acc,
-                                lhsT=hcodes[:, B * g:B * (g + 1)].bitcast(FP8X4),
-                                lhsT_scale=hscales[:, B * g:B * (g + 1)],
+                                lhsT=codes[:, B * g:B * (g + 1)].bitcast(FP8X4),
+                                lhsT_scale=scales[:, B * g:B * (g + 1)],
                                 rhs=rhs.bitcast(FP8X4), rhs_scale=rhs_scale,
-                                start=(g == 0), stop=(g == GD - 1))
+                                start=start, stop=stop)
 
         with tc.tile_pool(name="s2", bufs=1) as s2:
             planes = s2.tile([P, 5, NP], F32)
@@ -192,31 +207,39 @@ def tile_classifiermodel_w_kernel(tc, features, roi, conv_w_words, conv_w_scales
                 acc = psum.tile([P, BANK], F32, tag="bank", name="b23acc%d" % j)
                 b23acc.append(acc)
             for g in range(GD):
-                for j in range(4):
+                for j in (0, 2, 1, 3):
                     head_pass(b23acc[j][:], g, b23_w[g][:, BANK * j:BANK * (j + 1)],
-                              bbox_scale(g, NP + BANK * j, BANK))
+                              bbox_scale(g, NP + BANK * j, BANK), g == 0, g == GD - 1)
 
             b1_w = []
             cls_w = []
 
             def load_b1(c):
-                w = wpool.tile([P, GD, CH], U32, tag="w12", bufs=4, name="b1w%d" % c, align_bytes=64)
+                p0, n = CHUNKS[c]
+                w = wpool.tile([P, GD, n], U32, tag="w6", bufs=8, name="b1w%d" % c, align_bytes=64)
                 nc.sync.dma_start(out=w[:].bitcast(I32),
-                                  in_=bbox_w_words[:, :, NP + CH * c:NP + CH * (c + 1), :]
+                                  in_=bbox_w_words[:, :, NP + p0:NP + p0 + n, :]
                                   .rearrange("g p n t -> p g (n t)").bitcast(I32))
                 b1_w.append(w)
 
             for c in range(PRE):
                 load_b1(c)
-            for g in range(GD):
+            for g in range(GD - 1):
                 w = wpool.tile([P, 2 * NP], U32, tag="w8", bufs=N8, name="clsw%d" % g, align_bytes=64)
                 nc.sync.dma_start(out=w[:].bitcast(I32), in_=words(cls_w_words[g]))
                 cls_w.append(w)
-            for c in range(PRE, NCH):
+            cls_last = []
+            for hf in range(2):
+                w = wpool.tile([P, 2, BANK], U32, tag="w4", bufs=2, name="clsl%d" % hf, align_bytes=64)
+                nc.sync.dma_start(out=w[:].bitcast(I32),
+                                  in_=cls_w_words[GD - 1].rearrange("p (s n) t -> p s (n t)", s=2)
+                                  [:, :, 4 * BANK * hf:4 * BANK * (hf + 1)].bitcast(I32))
+                cls_last.append(w)
+            for c in range(PRE, len(CHUNKS)):
                 load_b1(c)
 
             e = None
-            for j in range(4):
+            for j in (0, 2, 1, 3):
                 comp = 2 + j // 2
                 sl = slice(BANK * (j % 2), BANK * (j % 2 + 1))
                 u = s2.tile([P, BANK], F32, tag="u", bufs=3, name="u%d" % j)
@@ -231,11 +254,12 @@ def tile_classifiermodel_w_kernel(tc, features, roi, conv_w_words, conv_w_scales
             nc.scalar.activation(out=warm[:], in_=e[:, 0:1], func=ACT.Sigmoid)
 
             def x_chunk(c):
-                sl = slice(CH * c, CH * (c + 1))
-                acc = psum.tile([P, CH], F32, tag="bank", name="b1acc%d" % c)
+                p0, n = CHUNKS[c]
+                sl = slice(p0, p0 + n)
+                acc = psum.tile([P, n], F32, tag="bank", name="b1acc%d" % c)
                 for g in range(GD):
-                    head_pass(acc[:], g, b1_w[c][:, g, :], bbox_scale(g, CH * c, CH))
-                tx = s2.tile([P, CH], F32, tag="tx", bufs=2, name="tx%d" % c)
+                    head_pass(acc[:], g, b1_w[c][:, g, :], bbox_scale(g, p0, n), g == 0, g == GD - 1)
+                tx = s2.tile([P, n], F32, tag="tx", bufs=2, name="tx%d" % c)
                 nc.vector.scalar_tensor_tensor(out=tx[:], in0=acc[:], scalar=16.0, in1=roi_sb[:, sl, 3],
                                                op0=ALU.mult, op1=ALU.mult)
                 nc.vector.tensor_tensor(out=planes[:, 0, sl], in0=planes[:, 0, sl], in1=tx[:], op=ALU.subtract)
@@ -244,27 +268,33 @@ def tile_classifiermodel_w_kernel(tc, features, roi, conv_w_words, conv_w_scales
                 x_chunk(c)
 
             clsacc = []
-            for j in range(4):
-                acc = psum.tile([P, BANK], F32, tag="bank", name="clsacc%d" % j)
+            for hf in range(2):
+                acc = psum.tile([P, BANK], F32, tag="bank", name="clsacc%d" % hf)
                 clsacc.append(acc)
-            order = (2, 0, 3, 1)
-            for g in range(GD):
-                for j in order:
-                    head_pass(clsacc[j][:], g, cls_w[g][:, BANK * j:BANK * (j + 1)], cls_scale(g, BANK * j, BANK))
+            for g in range(GD - 1):
+                for hf in range(2):
+                    head_pass(clsacc[hf][:], g, cls_w[g][:, NP + BANK * hf:NP + BANK * (hf + 1)],
+                              cls_scale(g, NP + BANK * hf, BANK), g == 0, False)
+                    head_pass(clsacc[hf][:], g, cls_w[g][:, BANK * hf:BANK * (hf + 1)],
+                              cls_scale(g, BANK * hf, BANK), False, False, negated=True)
             for hf in range(2):
                 sl = slice(BANK * hf, BANK * (hf + 1))
+                head_pass(clsacc[hf][:], GD - 1, cls_last[hf][:, 1, :], cls_scale(GD - 1, NP + BANK * hf, BANK),
+                          False, False)
+                head_pass(clsacc[hf][:], GD - 1, cls_last[hf][:, 0, :], cls_scale(GD - 1, BANK * hf, BANK),
+                          False, True, negated=True)
                 d = s2.tile([P, BANK], F32, tag="d", bufs=2, name="d%d" % hf)
-                nc.vector.tensor_tensor(out=d[:], in0=clsacc[2 + hf][:], in1=dbias[:, sl], op=ALU.add)
-                nc.vector.tensor_tensor(out=d[:], in0=d[:], in1=clsacc[hf][:], op=ALU.subtract)
+                nc.vector.tensor_tensor(out=d[:], in0=clsacc[hf][:], in1=dbias[:, sl], op=ALU.add)
                 nc.scalar.activation(out=planes[:, 4, sl], in_=d[:], func=ACT.Sigmoid)
 
-            for c in range(NCH):
+            for c in range(len(CHUNKS)):
                 if c >= PRE:
                     x_chunk(c)
-                sl = slice(CH * c, CH * (c + 1))
-                ob = s2.tile([P, CH, 5], F32, tag="ob", bufs=4, name="ob%d" % c)
-                if c % 2 == 0:
-                    nc.vector.tensor_copy(out=ob[:], in_=planes[:, :, sl].rearrange("p c n -> p n c"))
-                else:
+                p0, n = CHUNKS[c]
+                sl = slice(p0, p0 + n)
+                ob = s2.tile([P, n, 5], F32, tag="ob", bufs=5, name="ob%d" % c)
+                if c in COPY_ON_SCALAR:
                     nc.scalar.copy(out=ob[:], in_=planes[:, :, sl].rearrange("p c n -> p n c"))
+                else:
+                    nc.vector.tensor_copy(out=ob[:], in_=planes[:, :, sl].rearrange("p c n -> p n c"))
                 nc.sync.dma_start(out=out[:, sl, :], in_=ob[:])

@@ -109,17 +109,17 @@ def tile_classifiermodel_w_kernel(tc, features, roi, conv_w_words, conv_w_scales
                     conv_w.append(w)
             nc.sync.dma_start(out=roi_sb[:], in_=roi)
             for q in range(4):
-                nc.sync.dma_start(out=bbox_pl[32 * q:32 * q + 16, :].bitcast(I32),
-                                  in_=bbox_w_scales[0:4, 4 * q:4 * q + 4, NP:4 * NP].bitcast(I32))
+                nc.gpsimd.dma_start(out=bbox_pl[32 * q:32 * q + 16, :].bitcast(F32),
+                                  in_=bbox_w_scales[0:4, 4 * q:4 * q + 4, NP:4 * NP].bitcast(F32))
             for q in range(4):
-                nc.sync.dma_start(out=mix_pl[32 * q + 8:32 * q + 16, :].bitcast(I32),
-                                  in_=bbox_w_scales[4:6, 4 * q:4 * q + 4, NP:4 * NP].bitcast(I32))
+                nc.gpsimd.dma_start(out=mix_pl[32 * q + 8:32 * q + 16, :].bitcast(F32),
+                                  in_=bbox_w_scales[4:6, 4 * q:4 * q + 4, NP:4 * NP].bitcast(F32))
             for q in range(4):
-                nc.sync.dma_start(out=cls_pl[32 * q:32 * q + 16, :].bitcast(I32),
-                                  in_=cls_w_scales[0:4, 4 * q:4 * q + 4, :].bitcast(I32))
+                nc.gpsimd.dma_start(out=cls_pl[32 * q:32 * q + 16, :].bitcast(F32),
+                                  in_=cls_w_scales[0:4, 4 * q:4 * q + 4, :].bitcast(F32))
             for q in range(4):
-                nc.sync.dma_start(out=mix_pl[32 * q:32 * q + 8, 0:2 * NP].bitcast(I32),
-                                  in_=cls_w_scales[4:6, 4 * q:4 * q + 4, :].bitcast(I32))
+                nc.gpsimd.dma_start(out=mix_pl[32 * q:32 * q + 8, 0:2 * NP].bitcast(F32),
+                                  in_=cls_w_scales[4:6, 4 * q:4 * q + 4, :].bitcast(F32))
             b23_w = []
             for g in range(GD):
                 w = wpool.tile([P, 2 * NP], U32, tag="w8", bufs=N8, name="b23w%d" % g, align_bytes=64)

@@ -20,11 +20,8 @@ NP = 1024
 GC = C // 512
 GD = D // 512
 BANK = 512
-HALF = D // 2
-CHUNKS = ((0, 256), (256, 256), (512, 256), (768, 128), (896, 128))
-PRE = 1
-COPY_ON_SCALAR = (2,)
-N8 = 8
+NB = 5 * BANK
+CH = 256
 
 FLOPS = 2 * B * (C * D + D * 2 * NP + D * 3 * NP)
 BYTES = (B * C * 2 + B * NP * 4 * 2 + C * D + C * D // 32 + D * 2 + D * 2 * NP + D * 2 * NP // 32 + 2 * NP * 2
@@ -101,12 +98,10 @@ def tile_classifiermodel_w_kernel(tc, features, roi, conv_w_words, conv_w_scales
                 nc.sync.dma_start(out=conv_pl[32 * q:32 * q + 16, :].bitcast(I32),
                                   in_=conv_w_scales[:, 4 * q:4 * q + 4, :].bitcast(I32))
             conv_w = []
-            for hf in range(2):
-                for g in range(GC):
-                    w = wpool.tile([P, HALF], U32, tag="w6", bufs=8, name="convw%d_%d" % (hf, g), align_bytes=64)
-                    nc.sync.dma_start(out=w[:].bitcast(I32),
-                                      in_=words(conv_w_words[g][:, HALF * hf:HALF * (hf + 1), :]))
-                    conv_w.append(w)
+            for g in range(GC):
+                w = wpool.tile([P, D], U32, tag="w12", bufs=9, name="convw%d" % g, align_bytes=64)
+                nc.sync.dma_start(out=w[:].bitcast(I32), in_=words(conv_w_words[g]))
+                conv_w.append(w)
             nc.sync.dma_start(out=roi_sb[:], in_=roi)
             for q in range(4):
                 nc.gpsimd.dma_start(out=bbox_pl[32 * q:32 * q + 16, :].bitcast(F32),
@@ -120,11 +115,15 @@ def tile_classifiermodel_w_kernel(tc, features, roi, conv_w_words, conv_w_scales
             for q in range(4):
                 nc.gpsimd.dma_start(out=mix_pl[32 * q:32 * q + 8, 0:2 * NP].bitcast(F32),
                                   in_=cls_w_scales[4:6, 4 * q:4 * q + 4, :].bitcast(F32))
-            b23_w = []
-            for g in range(GD):
-                w = wpool.tile([P, 2 * NP], U32, tag="w8", bufs=N8, name="b23w%d" % g, align_bytes=64)
-                nc.sync.dma_start(out=w[:].bitcast(I32), in_=words(bbox_w_words[g][:, 2 * NP:4 * NP, :]))
-                b23_w.append(w)
+            b_w = []
+
+            def load_b(g):
+                w = wpool.tile([P, NB], U32, tag="w12", bufs=9, name="bw%d" % g, align_bytes=64)
+                nc.sync.dma_start(out=w[:].bitcast(I32), in_=words(bbox_w_words[g][:, 4 * NP - NB:4 * NP, :]))
+                b_w.append(w)
+
+            for g in range(5):
+                load_b(g)
 
             x32 = x_sb[:].bitcast(F32)
             fgrouped = s1.tile([P, C], BF16, align_bytes=64)
@@ -142,45 +141,42 @@ def tile_classifiermodel_w_kernel(tc, features, roi, conv_w_words, conv_w_scales
             for r in range(6):
                 spread_bias(r, cbias[:, BANK * r:BANK * (r + 1)], r % 2 == 0)
 
-            for hf in range(2):
-                hacc = []
-                for jj in range(3):
-                    acc = psum.tile([P, BANK], F32, tag="bank", name="hacc%d_%d" % (hf, jj))
-                    hacc.append(acc)
-                for g in range(GC):
-                    for jj in range(3):
-                        j = 3 * hf + jj
-                        nc.tensor.matmul_mx(out=hacc[jj][:],
-                                            lhsT=fcodes[:, B * g:B * (g + 1)].bitcast(FP8X4),
-                                            lhsT_scale=fscales[:, B * g:B * (g + 1)],
-                                            rhs=conv_w[GC * hf + g][:, BANK * jj:BANK * (jj + 1)].bitcast(FP8X4),
-                                            rhs_scale=conv_pl[4 * g:P, BANK * j:BANK * (j + 1)],
-                                            start=(g == 0), stop=(g == GC - 1))
-                if hf == 0:
-                    for r in range(6, 12):
-                        spread_bias(r, bbias[:, BANK * (r - 6):BANK * (r - 5)], r % 2 == 0)
-                    for r in range(12, 14):
-                        spread_bias(r, dbias[:, BANK * (r - 12):BANK * (r - 11)], r % 2 == 0)
-                for jj in range(3):
-                    j = 3 * hf + jj
-                    tmp = s1.tile([P, BANK], F32, tag="tmp", bufs=3, name="tmp%d" % j)
-                    nc.vector.tensor_tensor(out=tmp[:], in0=hacc[jj][:], in1=cbias[:, BANK * j:BANK * (j + 1)],
-                                            op=ALU.add)
-                    hperm = s1.tile([P, 4, P], BF16, tag="hperm", bufs=3, name="hperm%d" % j)
-                    nc.scalar.activation(out=hperm[:], in_=tmp[:].rearrange("p (q t) -> p t q", t=4), func=ACT.Relu)
-                    ht = psum.tile([P, 4, B], BF16, tag="bank", name="ht%d" % j)
-                    for t in range(4):
-                        nc.tensor.transpose(ht[:, t, :], hperm[:, t, :], ident_b[:])
-                    hg = s1.tile([P, B, 4], BF16, tag="hg", bufs=3, name="hg%d" % j, align_bytes=64)
-                    nc.vector.tensor_copy(out=hg[:], in_=ht[:].rearrange("p t b -> p b t"))
-                    hgn = s1.tile([P, B, 4], BF16, tag="hgn", bufs=3, name="hgn%d" % j, align_bytes=64)
-                    nc.scalar.activation(out=hgn[:], in_=ht[:].rearrange("p t b -> p b t"), func=ACT.Copy, scale=-1.0)
-                    nc.vector.quantize_mx(out=hcodes[:, B * j:B * (j + 1)].bitcast(FP8X4),
-                                          scales=hscales[:, B * j:B * (j + 1)],
-                                          in_=hg[:].rearrange("p b t -> p (b t)"))
-                    nc.vector.quantize_mx(out=ncodes[:, B * j:B * (j + 1)].bitcast(FP8X4),
-                                          scales=nscales[:, B * j:B * (j + 1)],
-                                          in_=hgn[:].rearrange("p b t -> p (b t)"))
+            hacc = []
+            for j in range(GD):
+                acc = psum.tile([P, BANK], F32, tag="bank", name="hacc%d" % j)
+                hacc.append(acc)
+            for g in range(GC):
+                for j in range(GD):
+                    nc.tensor.matmul_mx(out=hacc[j][:],
+                                        lhsT=fcodes[:, B * g:B * (g + 1)].bitcast(FP8X4),
+                                        lhsT_scale=fscales[:, B * g:B * (g + 1)],
+                                        rhs=conv_w[g][:, BANK * j:BANK * (j + 1)].bitcast(FP8X4),
+                                        rhs_scale=conv_pl[4 * g:P, BANK * j:BANK * (j + 1)],
+                                        start=(g == 0), stop=(g == GC - 1))
+            load_b(5)
+            for j in range(GD):
+                tmp = s1.tile([P, BANK], F32, tag="tmp", bufs=3, name="tmp%d" % j)
+                nc.vector.tensor_tensor(out=tmp[:], in0=hacc[j][:], in1=cbias[:, BANK * j:BANK * (j + 1)],
+                                        op=ALU.add)
+                hperm = s1.tile([P, 4, P], BF16, tag="hperm", bufs=3, name="hperm%d" % j)
+                nc.scalar.activation(out=hperm[:], in_=tmp[:].rearrange("p (q t) -> p t q", t=4), func=ACT.Relu)
+                ht = psum.tile([P, 4, B], BF16, tag="bank", name="ht%d" % j)
+                for t in range(4):
+                    nc.tensor.transpose(ht[:, t, :], hperm[:, t, :], ident_b[:])
+                hg = s1.tile([P, B, 4], BF16, tag="hg", bufs=3, name="hg%d" % j, align_bytes=64)
+                nc.vector.tensor_copy(out=hg[:], in_=ht[:].rearrange("p t b -> p b t"))
+                hgn = s1.tile([P, B, 4], BF16, tag="hgn", bufs=3, name="hgn%d" % j, align_bytes=64)
+                nc.scalar.activation(out=hgn[:], in_=ht[:].rearrange("p t b -> p b t"), func=ACT.Copy, scale=-1.0)
+                nc.vector.quantize_mx(out=hcodes[:, B * j:B * (j + 1)].bitcast(FP8X4),
+                                      scales=hscales[:, B * j:B * (j + 1)],
+                                      in_=hg[:].rearrange("p b t -> p (b t)"))
+                nc.vector.quantize_mx(out=ncodes[:, B * j:B * (j + 1)].bitcast(FP8X4),
+                                      scales=nscales[:, B * j:B * (j + 1)],
+                                      in_=hgn[:].rearrange("p b t -> p (b t)"))
+            for r in range(6, 12):
+                spread_bias(r, bbias[:, BANK * (r - 6):BANK * (r - 5)], r % 2 == 0)
+            for r in range(12, 14):
+                spread_bias(r, dbias[:, BANK * (r - 12):BANK * (r - 11)], r % 2 == 0)
 
         def head_pass(acc, g, rhs, rhs_scale, start, stop, negated=False):
             codes = ncodes if negated else hcodes
@@ -202,48 +198,55 @@ def tile_classifiermodel_w_kernel(tc, features, roi, conv_w_words, conv_w_scales
                 nc.vector.scalar_tensor_tensor(out=planes[:, 0, sl], in0=roi_sb[:, sl, 0], scalar=16.0, in1=m[:],
                                                op0=ALU.mult, op1=ALU.subtract)
 
-            b23acc = []
-            for j in range(4):
-                acc = psum.tile([P, BANK], F32, tag="bank", name="b23acc%d" % j)
-                b23acc.append(acc)
+            bacc = []
+            for k in range(5):
+                acc = psum.tile([P, BANK], F32, tag="bank", name="bacc%d" % k)
+                bacc.append(acc)
             for g in range(GD):
-                for j in (0, 2, 1, 3):
-                    head_pass(b23acc[j][:], g, b23_w[g][:, BANK * j:BANK * (j + 1)],
-                              bbox_scale(g, NP + BANK * j, BANK), g == 0, g == GD - 1)
+                for k in range(5):
+                    head_pass(bacc[k][:], g, b_w[g][:, BANK * k:BANK * (k + 1)],
+                              bbox_scale(g, BANK * (k + 1), BANK), g == 0, g == GD - 1)
 
-            b1_w = []
             cls_w = []
-
-            def load_b1(c):
-                p0, n = CHUNKS[c]
-                w = wpool.tile([P, GD, n], U32, tag="w6", bufs=8, name="b1w%d" % c, align_bytes=64)
-                nc.sync.dma_start(out=w[:].bitcast(I32),
-                                  in_=bbox_w_words[:, :, NP + p0:NP + p0 + n, :]
-                                  .rearrange("g p n t -> p g (n t)").bitcast(I32))
-                b1_w.append(w)
-
-            for c in range(PRE):
-                load_b1(c)
             for g in range(GD - 1):
-                w = wpool.tile([P, 2 * NP], U32, tag="w8", bufs=N8, name="clsw%d" % g, align_bytes=64)
+                w = wpool.tile([P, 2 * NP], U32, tag="w12", bufs=9, name="clsw%d" % g, align_bytes=64)
                 nc.sync.dma_start(out=w[:].bitcast(I32), in_=words(cls_w_words[g]))
                 cls_w.append(w)
-            cls_last = []
-            for hf in range(2):
-                w = wpool.tile([P, 2, BANK], U32, tag="w4", bufs=2, name="clsl%d" % hf, align_bytes=64)
+            cls_last = {}
+            for hf in (1, 0):
+                w = wpool.tile([P, 2, BANK], U32, tag="w12", bufs=9, name="clsl%d" % hf, align_bytes=64)
                 nc.sync.dma_start(out=w[:].bitcast(I32),
                                   in_=cls_w_words[GD - 1].rearrange("p (s n) t -> p s (n t)", s=2)
                                   [:, :, 4 * BANK * hf:4 * BANK * (hf + 1)].bitcast(I32))
-                cls_last.append(w)
-            for c in range(PRE, len(CHUNKS)):
-                load_b1(c)
+                cls_last[hf] = w
+            x_w = {}
+            for g0, g1 in ((0, 4), (4, 6)):
+                w = wpool.tile([P, g1 - g0, BANK], U32, tag="w12", bufs=9, name="xw%d" % g0, align_bytes=64)
+                nc.sync.dma_start(out=w[:].bitcast(I32),
+                                  in_=bbox_w_words[g0:g1, :, NP:NP + BANK, :]
+                                  .rearrange("g p n t -> p g (n t)").bitcast(I32))
+                for g in range(g0, g1):
+                    x_w[g] = w[:, g - g0, :]
 
+            def x_out(acc, sl, n):
+                tx = s2.tile([P, n], F32, tag="tx", bufs=2, name="tx%d" % sl.start)
+                nc.vector.scalar_tensor_tensor(out=tx[:], in0=acc, scalar=16.0, in1=roi_sb[:, sl, 3],
+                                               op0=ALU.mult, op1=ALU.mult)
+                nc.vector.tensor_tensor(out=planes[:, 0, sl], in0=planes[:, 0, sl], in1=tx[:], op=ALU.subtract)
+
+            def store(c):
+                sl = slice(CH * c, CH * (c + 1))
+                ob = s2.tile([P, CH, 5], F32, tag="ob", bufs=4, name="ob%d" % c)
+                nc.vector.tensor_copy(out=ob[:], in_=planes[:, :, sl].rearrange("p c n -> p n c"))
+                nc.sync.dma_start(out=out[:, sl, :], in_=ob[:])
+
+            x_out(bacc[0][:], slice(BANK, NP), BANK)
             e = None
-            for j in (0, 2, 1, 3):
+            for j in range(4):
                 comp = 2 + j // 2
                 sl = slice(BANK * (j % 2), BANK * (j % 2 + 1))
                 u = s2.tile([P, BANK], F32, tag="u", bufs=3, name="u%d" % j)
-                nc.vector.tensor_tensor(out=u[:], in0=b23acc[j][:], in1=bbias[:, NP + BANK * j:NP + BANK * (j + 1)],
+                nc.vector.tensor_tensor(out=u[:], in0=bacc[j + 1][:], in1=bbias[:, NP + BANK * j:NP + BANK * (j + 1)],
                                         op=ALU.add)
                 nc.vector.tensor_scalar(out=u[:], in0=u[:], scalar1=10.0, scalar2=-10.0, op0=ALU.min, op1=ALU.max)
                 e = s2.tile([P, BANK], F32, tag="e", bufs=3, name="e%d" % j)
@@ -252,20 +255,6 @@ def tile_classifiermodel_w_kernel(tc, features, roi, conv_w_words, conv_w_scales
                                                op0=ALU.mult, op1=ALU.mult)
             warm = s2.tile([P, 1], F32)
             nc.scalar.activation(out=warm[:], in_=e[:, 0:1], func=ACT.Sigmoid)
-
-            def x_chunk(c):
-                p0, n = CHUNKS[c]
-                sl = slice(p0, p0 + n)
-                acc = psum.tile([P, n], F32, tag="bank", name="b1acc%d" % c)
-                for g in range(GD):
-                    head_pass(acc[:], g, b1_w[c][:, g, :], bbox_scale(g, p0, n), g == 0, g == GD - 1)
-                tx = s2.tile([P, n], F32, tag="tx", bufs=2, name="tx%d" % c)
-                nc.vector.scalar_tensor_tensor(out=tx[:], in0=acc[:], scalar=16.0, in1=roi_sb[:, sl, 3],
-                                               op0=ALU.mult, op1=ALU.mult)
-                nc.vector.tensor_tensor(out=planes[:, 0, sl], in0=planes[:, 0, sl], in1=tx[:], op=ALU.subtract)
-
-            for c in range(PRE):
-                x_chunk(c)
 
             clsacc = []
             for hf in range(2):
@@ -277,24 +266,30 @@ def tile_classifiermodel_w_kernel(tc, features, roi, conv_w_words, conv_w_scales
                               cls_scale(g, NP + BANK * hf, BANK), g == 0, False)
                     head_pass(clsacc[hf][:], g, cls_w[g][:, BANK * hf:BANK * (hf + 1)],
                               cls_scale(g, BANK * hf, BANK), False, False, negated=True)
-            for hf in range(2):
-                sl = slice(BANK * hf, BANK * (hf + 1))
+            for hf in (1, 0):
                 head_pass(clsacc[hf][:], GD - 1, cls_last[hf][:, 1, :], cls_scale(GD - 1, NP + BANK * hf, BANK),
                           False, False)
                 head_pass(clsacc[hf][:], GD - 1, cls_last[hf][:, 0, :], cls_scale(GD - 1, BANK * hf, BANK),
                           False, True, negated=True)
-                d = s2.tile([P, BANK], F32, tag="d", bufs=2, name="d%d" % hf)
-                nc.vector.tensor_tensor(out=d[:], in0=clsacc[hf][:], in1=dbias[:, sl], op=ALU.add)
-                nc.scalar.activation(out=planes[:, 4, sl], in_=d[:], func=ACT.Sigmoid)
+                for c in (2 * hf, 2 * hf + 1):
+                    off = CH * (c - 2 * hf)
+                    d = s2.tile([P, CH], F32, tag="d", bufs=2, name="d%d" % c)
+                    nc.vector.tensor_tensor(out=d[:], in0=clsacc[hf][:, off:off + CH],
+                                            in1=dbias[:, CH * c:CH * (c + 1)], op=ALU.add)
+                    nc.scalar.activation(out=planes[:, 4, CH * c:CH * (c + 1)], in_=d[:], func=ACT.Sigmoid)
+                    if hf == 1:
+                        store(c)
 
-            for c in range(len(CHUNKS)):
-                if c >= PRE:
-                    x_chunk(c)
-                p0, n = CHUNKS[c]
-                sl = slice(p0, p0 + n)
-                ob = s2.tile([P, n, 5], F32, tag="ob", bufs=5, name="ob%d" % c)
-                if c in COPY_ON_SCALAR:
-                    nc.scalar.copy(out=ob[:], in_=planes[:, :, sl].rearrange("p c n -> p n c"))
-                else:
-                    nc.vector.tensor_copy(out=ob[:], in_=planes[:, :, sl].rearrange("p c n -> p n c"))
-                nc.sync.dma_start(out=out[:, sl, :], in_=ob[:])
+            xacc = []
+            for c in range(2):
+                acc = psum.tile([P, CH], F32, tag="bank", name="xacc%d" % c)
+                xacc.append(acc)
+            for g in range(4):
+                for c in range(2):
+                    head_pass(xacc[c][:], g, x_w[g][:, CH * c:CH * (c + 1)], bbox_scale(g, CH * c, CH), g == 0, False)
+            for c in range(2):
+                for g in range(4, GD):
+                    head_pass(xacc[c][:], g, x_w[g][:, CH * c:CH * (c + 1)], bbox_scale(g, CH * c, CH),
+                              False, g == GD - 1)
+                x_out(xacc[c][:], slice(CH * c, CH * (c + 1)), CH)
+                store(c)

@@ -91,17 +91,22 @@ def tile_classifiermodel_w_kernel(tc, features, roi, conv_w_words, conv_w_scales
         with tc.tile_pool(name="s1", bufs=1) as s1:
             x_sb = s1.tile([P, C], BF16)
             nc.sync.dma_start(out=x_sb[:], in_=features.rearrange("b h w c -> b (h w c)"))
-            nc.scalar.dma_start(out=brow[0:6, :], in_=conv_b.rearrange("(r c) -> r c", c=BANK))
-            nc.scalar.dma_start(out=brow[6:12, :], in_=bbox_b[NP:4 * NP].rearrange("(r c) -> r c", c=BANK))
-            nc.scalar.dma_start(out=brow[12:16, :], in_=cls_b.rearrange("(r c) -> r c", c=BANK))
+            conv_w = []
+
+            def load_conv(g):
+                w = wpool.tile([P, D], U32, tag="w12", bufs=8, name="convw%d" % g, align_bytes=64)
+                nc.sync.dma_start(out=w[:].bitcast(I32), in_=words(conv_w_words[g]))
+                conv_w.append(w)
+
+            load_conv(0)
             for q in range(4):
                 nc.sync.dma_start(out=conv_pl[32 * q:32 * q + 16, :].bitcast(I32),
                                   in_=conv_w_scales[:, 4 * q:4 * q + 4, :].bitcast(I32))
-            conv_w = []
-            for g in range(GC):
-                w = wpool.tile([P, D], U32, tag="w12", bufs=9, name="convw%d" % g, align_bytes=64)
-                nc.sync.dma_start(out=w[:].bitcast(I32), in_=words(conv_w_words[g]))
-                conv_w.append(w)
+            for g in range(1, GC):
+                load_conv(g)
+            nc.gpsimd.dma_start(out=brow[0:6, :], in_=conv_b.rearrange("(r c) -> r c", c=BANK))
+            nc.gpsimd.dma_start(out=brow[6:12, :], in_=bbox_b[NP:4 * NP].rearrange("(r c) -> r c", c=BANK))
+            nc.gpsimd.dma_start(out=brow[12:16, :], in_=cls_b.rearrange("(r c) -> r c", c=BANK))
             nc.sync.dma_start(out=roi_sb[:], in_=roi)
             for q in range(4):
                 nc.gpsimd.dma_start(out=bbox_pl[32 * q:32 * q + 16, :].bitcast(F32),
@@ -110,19 +115,19 @@ def tile_classifiermodel_w_kernel(tc, features, roi, conv_w_words, conv_w_scales
                 nc.gpsimd.dma_start(out=mix_pl[32 * q + 8:32 * q + 16, :].bitcast(F32),
                                   in_=bbox_w_scales[4:6, 4 * q:4 * q + 4, NP:4 * NP].bitcast(F32))
             for q in range(4):
-                nc.gpsimd.dma_start(out=cls_pl[32 * q:32 * q + 16, :].bitcast(F32),
-                                  in_=cls_w_scales[0:4, 4 * q:4 * q + 4, :].bitcast(F32))
-            for q in range(4):
                 nc.gpsimd.dma_start(out=mix_pl[32 * q:32 * q + 8, 0:2 * NP].bitcast(F32),
                                   in_=cls_w_scales[4:6, 4 * q:4 * q + 4, :].bitcast(F32))
+            for q in range(4):
+                nc.gpsimd.dma_start(out=cls_pl[32 * q:32 * q + 16, :].bitcast(F32),
+                                  in_=cls_w_scales[0:4, 4 * q:4 * q + 4, :].bitcast(F32))
             b_w = []
 
             def load_b(g):
-                w = wpool.tile([P, NB], U32, tag="w12", bufs=9, name="bw%d" % g, align_bytes=64)
+                w = wpool.tile([P, NB], U32, tag="w12", bufs=8, name="bw%d" % g, align_bytes=64)
                 nc.sync.dma_start(out=w[:].bitcast(I32), in_=words(bbox_w_words[g][:, 4 * NP - NB:4 * NP, :]))
                 b_w.append(w)
 
-            for g in range(5):
+            for g in range(4):
                 load_b(g)
 
             x32 = x_sb[:].bitcast(F32)
@@ -153,7 +158,8 @@ def tile_classifiermodel_w_kernel(tc, features, roi, conv_w_words, conv_w_scales
                                         rhs=conv_w[g][:, BANK * j:BANK * (j + 1)].bitcast(FP8X4),
                                         rhs_scale=conv_pl[4 * g:P, BANK * j:BANK * (j + 1)],
                                         start=(g == 0), stop=(g == GC - 1))
-            load_b(5)
+            for g in range(4, GD):
+                load_b(g)
             for j in range(GD):
                 tmp = s1.tile([P, BANK], F32, tag="tmp", bufs=3, name="tmp%d" % j)
                 nc.vector.tensor_tensor(out=tmp[:], in0=hacc[j][:], in1=cbias[:, BANK * j:BANK * (j + 1)],
@@ -209,19 +215,19 @@ def tile_classifiermodel_w_kernel(tc, features, roi, conv_w_words, conv_w_scales
 
             cls_w = []
             for g in range(GD - 1):
-                w = wpool.tile([P, 2 * NP], U32, tag="w12", bufs=9, name="clsw%d" % g, align_bytes=64)
+                w = wpool.tile([P, 2 * NP], U32, tag="w12", bufs=8, name="clsw%d" % g, align_bytes=64)
                 nc.sync.dma_start(out=w[:].bitcast(I32), in_=words(cls_w_words[g]))
                 cls_w.append(w)
             cls_last = {}
             for hf in (1, 0):
-                w = wpool.tile([P, 2, BANK], U32, tag="w12", bufs=9, name="clsl%d" % hf, align_bytes=64)
+                w = wpool.tile([P, 2, BANK], U32, tag="tail", bufs=4, name="clsl%d" % hf, align_bytes=64)
                 nc.sync.dma_start(out=w[:].bitcast(I32),
                                   in_=cls_w_words[GD - 1].rearrange("p (s n) t -> p s (n t)", s=2)
                                   [:, :, 4 * BANK * hf:4 * BANK * (hf + 1)].bitcast(I32))
                 cls_last[hf] = w
             x_w = {}
             for g0, g1 in ((0, 4), (4, 6)):
-                w = wpool.tile([P, g1 - g0, BANK], U32, tag="w12", bufs=9, name="xw%d" % g0, align_bytes=64)
+                w = wpool.tile([P, g1 - g0, BANK], U32, tag="tail", bufs=4, name="xw%d" % g0, align_bytes=64)
                 nc.sync.dma_start(out=w[:].bitcast(I32),
                                   in_=bbox_w_words[g0:g1, :, NP:NP + BANK, :]
                                   .rearrange("g p n t -> p g (n t)").bitcast(I32))

@@ -60,8 +60,6 @@ def tile_classifiermodel_w_kernel(tc, features, roi, conv_w_words, conv_w_scales
         fscales = const.tile([P, GC * B], U8, align_bytes=64)
         hcodes = const.tile([P, GD * B], U32, align_bytes=64)
         hscales = const.tile([P, GD * B], U8, align_bytes=64)
-        ncodes = const.tile([P, GD * B], U32, align_bytes=64)
-        nscales = const.tile([P, GD * B], U8, align_bytes=64)
         bbias = const.tile([P, 3 * NP], BF16)
         dbias = const.tile([P, NP], F32)
         roi_sb = const.tile([P, NP, 4], BF16)
@@ -104,22 +102,9 @@ def tile_classifiermodel_w_kernel(tc, features, roi, conv_w_words, conv_w_scales
                                   in_=conv_w_scales[:, 4 * q:4 * q + 4, :].bitcast(I32))
             for g in range(1, GC):
                 load_conv(g)
-            nc.gpsimd.dma_start(out=brow[0:6, :], in_=conv_b.rearrange("(r c) -> r c", c=BANK))
-            nc.gpsimd.dma_start(out=brow[6:12, :], in_=bbox_b[NP:4 * NP].rearrange("(r c) -> r c", c=BANK))
-            nc.gpsimd.dma_start(out=brow[12:16, :], in_=cls_b.rearrange("(r c) -> r c", c=BANK))
-            nc.sync.dma_start(out=roi_sb[:], in_=roi)
-            for q in range(4):
-                nc.gpsimd.dma_start(out=bbox_pl[32 * q:32 * q + 16, :].bitcast(F32),
-                                  in_=bbox_w_scales[0:4, 4 * q:4 * q + 4, NP:4 * NP].bitcast(F32))
-            for q in range(4):
-                nc.gpsimd.dma_start(out=mix_pl[32 * q + 8:32 * q + 16, :].bitcast(F32),
-                                  in_=bbox_w_scales[4:6, 4 * q:4 * q + 4, NP:4 * NP].bitcast(F32))
-            for q in range(4):
-                nc.gpsimd.dma_start(out=mix_pl[32 * q:32 * q + 8, 0:2 * NP].bitcast(F32),
-                                  in_=cls_w_scales[4:6, 4 * q:4 * q + 4, :].bitcast(F32))
-            for q in range(4):
-                nc.gpsimd.dma_start(out=cls_pl[32 * q:32 * q + 16, :].bitcast(F32),
-                                  in_=cls_w_scales[0:4, 4 * q:4 * q + 4, :].bitcast(F32))
+            nc.scalar.dma_start(out=brow[0:6, :], in_=conv_b.rearrange("(r c) -> r c", c=BANK))
+            nc.scalar.dma_start(out=brow[6:12, :], in_=bbox_b[NP:4 * NP].rearrange("(r c) -> r c", c=BANK))
+            nc.scalar.dma_start(out=brow[12:16, :], in_=cls_b.rearrange("(r c) -> r c", c=BANK))
             b_w = []
 
             def load_b(g):
@@ -127,8 +112,21 @@ def tile_classifiermodel_w_kernel(tc, features, roi, conv_w_words, conv_w_scales
                 nc.sync.dma_start(out=w[:].bitcast(I32), in_=words(bbox_w_words[g][:, 4 * NP - NB:4 * NP, :]))
                 b_w.append(w)
 
-            for g in range(4):
-                load_b(g)
+            def load_scales(plane, first, scales, g0, g1, n0, n1):
+                for q in range(4):
+                    rows = slice(32 * q + first, 32 * q + first + 4 * (g1 - g0))
+                    nc.sync.dma_start(out=plane[rows, 0:n1 - n0].bitcast(I32),
+                                      in_=scales[g0:g1, 4 * q:4 * q + 4, n0:n1].bitcast(I32))
+
+            load_scales(bbox_pl, 0, bbox_w_scales, 0, 4, NP, 4 * NP)
+            load_b(0)
+            load_scales(mix_pl, 8, bbox_w_scales, 4, 6, NP, 4 * NP)
+            load_b(1)
+            load_scales(mix_pl, 0, cls_w_scales, 4, 6, 0, 2 * NP)
+            load_b(2)
+            load_scales(cls_pl, 0, cls_w_scales, 0, 4, 0, 2 * NP)
+            load_b(3)
+            nc.sync.dma_start(out=roi_sb[:], in_=roi)
 
             x32 = x_sb[:].bitcast(F32)
             fgrouped = s1.tile([P, C], BF16, align_bytes=64)
@@ -171,25 +169,18 @@ def tile_classifiermodel_w_kernel(tc, features, roi, conv_w_words, conv_w_scales
                     nc.tensor.transpose(ht[:, t, :], hperm[:, t, :], ident_b[:])
                 hg = s1.tile([P, B, 4], BF16, tag="hg", bufs=3, name="hg%d" % j, align_bytes=64)
                 nc.vector.tensor_copy(out=hg[:], in_=ht[:].rearrange("p t b -> p b t"))
-                hgn = s1.tile([P, B, 4], BF16, tag="hgn", bufs=3, name="hgn%d" % j, align_bytes=64)
-                nc.scalar.activation(out=hgn[:], in_=ht[:].rearrange("p t b -> p b t"), func=ACT.Copy, scale=-1.0)
                 nc.vector.quantize_mx(out=hcodes[:, B * j:B * (j + 1)].bitcast(FP8X4),
                                       scales=hscales[:, B * j:B * (j + 1)],
                                       in_=hg[:].rearrange("p b t -> p (b t)"))
-                nc.vector.quantize_mx(out=ncodes[:, B * j:B * (j + 1)].bitcast(FP8X4),
-                                      scales=nscales[:, B * j:B * (j + 1)],
-                                      in_=hgn[:].rearrange("p b t -> p (b t)"))
             for r in range(6, 12):
                 spread_bias(r, bbias[:, BANK * (r - 6):BANK * (r - 5)], r % 2 == 0)
             for r in range(12, 14):
                 spread_bias(r, dbias[:, BANK * (r - 12):BANK * (r - 11)], r % 2 == 0)
 
-        def head_pass(acc, g, rhs, rhs_scale, start, stop, negated=False):
-            codes = ncodes if negated else hcodes
-            scales = nscales if negated else hscales
+        def head_pass(acc, g, rhs, rhs_scale, start, stop):
             nc.tensor.matmul_mx(out=acc,
-                                lhsT=codes[:, B * g:B * (g + 1)].bitcast(FP8X4),
-                                lhsT_scale=scales[:, B * g:B * (g + 1)],
+                                lhsT=hcodes[:, B * g:B * (g + 1)].bitcast(FP8X4),
+                                lhsT_scale=hscales[:, B * g:B * (g + 1)],
                                 rhs=rhs.bitcast(FP8X4), rhs_scale=rhs_scale,
                                 start=start, stop=stop)
 
@@ -198,7 +189,7 @@ def tile_classifiermodel_w_kernel(tc, features, roi, conv_w_words, conv_w_scales
             nc.scalar.activation(out=planes[:, 1, :], in_=roi_sb[:, :, 1], func=ACT.Copy, scale=16.0)
             for hf in range(2):
                 sl = slice(BANK * hf, BANK * (hf + 1))
-                m = s2.tile([P, BANK], F32, tag="u", bufs=3, name="m%d" % hf)
+                m = s2.tile([P, BANK], F32, tag="u", bufs=2, name="m%d" % hf)
                 nc.vector.scalar_tensor_tensor(out=m[:], in0=bbias[:, sl], scalar=16.0, in1=roi_sb[:, sl, 3],
                                                op0=ALU.mult, op1=ALU.mult)
                 nc.vector.scalar_tensor_tensor(out=planes[:, 0, sl], in0=roi_sb[:, sl, 0], scalar=16.0, in1=m[:],
@@ -218,16 +209,17 @@ def tile_classifiermodel_w_kernel(tc, features, roi, conv_w_words, conv_w_scales
                 w = wpool.tile([P, 2 * NP], U32, tag="w12", bufs=8, name="clsw%d" % g, align_bytes=64)
                 nc.sync.dma_start(out=w[:].bitcast(I32), in_=words(cls_w_words[g]))
                 cls_w.append(w)
-            cls_last = {}
+            c0_last = wpool.tile([P, NP], U32, tag="tail", bufs=5, name="c0l", align_bytes=64)
+            nc.sync.dma_start(out=c0_last[:].bitcast(I32), in_=words(cls_w_words[GD - 1][:, 0:NP, :]))
+            c1_last = {}
             for hf in (1, 0):
-                w = wpool.tile([P, 2, BANK], U32, tag="tail", bufs=4, name="clsl%d" % hf, align_bytes=64)
+                w = wpool.tile([P, BANK], U32, tag="tail", bufs=5, name="c1l%d" % hf, align_bytes=64)
                 nc.sync.dma_start(out=w[:].bitcast(I32),
-                                  in_=cls_w_words[GD - 1].rearrange("p (s n) t -> p s (n t)", s=2)
-                                  [:, :, 4 * BANK * hf:4 * BANK * (hf + 1)].bitcast(I32))
-                cls_last[hf] = w
+                                  in_=words(cls_w_words[GD - 1][:, NP + BANK * hf:NP + BANK * (hf + 1), :]))
+                c1_last[hf] = w
             x_w = {}
             for g0, g1 in ((0, 4), (4, 6)):
-                w = wpool.tile([P, g1 - g0, BANK], U32, tag="tail", bufs=4, name="xw%d" % g0, align_bytes=64)
+                w = wpool.tile([P, g1 - g0, BANK], U32, tag="tail", bufs=5, name="xw%d" % g0, align_bytes=64)
                 nc.sync.dma_start(out=w[:].bitcast(I32),
                                   in_=bbox_w_words[g0:g1, :, NP:NP + BANK, :]
                                   .rearrange("g p n t -> p g (n t)").bitcast(I32))
@@ -251,37 +243,44 @@ def tile_classifiermodel_w_kernel(tc, features, roi, conv_w_words, conv_w_scales
             for j in range(4):
                 comp = 2 + j // 2
                 sl = slice(BANK * (j % 2), BANK * (j % 2 + 1))
-                u = s2.tile([P, BANK], F32, tag="u", bufs=3, name="u%d" % j)
+                u = s2.tile([P, BANK], F32, tag="u", bufs=2, name="u%d" % j)
                 nc.vector.tensor_tensor(out=u[:], in0=bacc[j + 1][:], in1=bbias[:, NP + BANK * j:NP + BANK * (j + 1)],
                                         op=ALU.add)
                 nc.vector.tensor_scalar(out=u[:], in0=u[:], scalar1=10.0, scalar2=-10.0, op0=ALU.min, op1=ALU.max)
-                e = s2.tile([P, BANK], F32, tag="e", bufs=3, name="e%d" % j)
+                e = s2.tile([P, BANK], F32, tag="e", bufs=2, name="e%d" % j)
                 nc.scalar.activation(out=e[:], in_=u[:], func=ACT.Exp)
                 nc.vector.scalar_tensor_tensor(out=planes[:, comp, sl], in0=e[:], scalar=16.0, in1=roi_sb[:, sl, comp],
                                                op0=ALU.mult, op1=ALU.mult)
             warm = s2.tile([P, 1], F32)
             nc.scalar.activation(out=warm[:], in_=e[:, 0:1], func=ACT.Sigmoid)
 
-            clsacc = []
+            c0acc = []
+            c1acc = []
             for hf in range(2):
-                acc = psum.tile([P, BANK], F32, tag="bank", name="clsacc%d" % hf)
-                clsacc.append(acc)
+                acc = psum.tile([P, BANK], F32, tag="bank", name="c0acc%d" % hf)
+                c0acc.append(acc)
+            for hf in range(2):
+                acc = psum.tile([P, BANK], F32, tag="bank", name="c1acc%d" % hf)
+                c1acc.append(acc)
             for g in range(GD - 1):
                 for hf in range(2):
-                    head_pass(clsacc[hf][:], g, cls_w[g][:, NP + BANK * hf:NP + BANK * (hf + 1)],
+                    head_pass(c0acc[hf][:], g, cls_w[g][:, BANK * hf:BANK * (hf + 1)],
+                              cls_scale(g, BANK * hf, BANK), g == 0, False)
+                for hf in range(2):
+                    head_pass(c1acc[hf][:], g, cls_w[g][:, NP + BANK * hf:NP + BANK * (hf + 1)],
                               cls_scale(g, NP + BANK * hf, BANK), g == 0, False)
-                    head_pass(clsacc[hf][:], g, cls_w[g][:, BANK * hf:BANK * (hf + 1)],
-                              cls_scale(g, BANK * hf, BANK), False, False, negated=True)
+            e0 = s2.tile([P, NP], F32)
             for hf in (1, 0):
-                head_pass(clsacc[hf][:], GD - 1, cls_last[hf][:, 1, :], cls_scale(GD - 1, NP + BANK * hf, BANK),
-                          False, False)
-                head_pass(clsacc[hf][:], GD - 1, cls_last[hf][:, 0, :], cls_scale(GD - 1, BANK * hf, BANK),
-                          False, True, negated=True)
+                sl = slice(BANK * hf, BANK * (hf + 1))
+                head_pass(c0acc[hf][:], GD - 1, c0_last[:, sl], cls_scale(GD - 1, BANK * hf, BANK), False, True)
+                nc.vector.tensor_tensor(out=e0[:, sl], in0=c0acc[hf][:], in1=dbias[:, sl], op=ALU.subtract)
+            for hf in (1, 0):
+                head_pass(c1acc[hf][:], GD - 1, c1_last[hf][:], cls_scale(GD - 1, NP + BANK * hf, BANK), False, True)
                 for c in (2 * hf, 2 * hf + 1):
                     off = CH * (c - 2 * hf)
                     d = s2.tile([P, CH], F32, tag="d", bufs=2, name="d%d" % c)
-                    nc.vector.tensor_tensor(out=d[:], in0=clsacc[hf][:, off:off + CH],
-                                            in1=dbias[:, CH * c:CH * (c + 1)], op=ALU.add)
+                    nc.vector.tensor_tensor(out=d[:], in0=c1acc[hf][:, off:off + CH],
+                                            in1=e0[:, CH * c:CH * (c + 1)], op=ALU.subtract)
                     nc.scalar.activation(out=planes[:, 4, CH * c:CH * (c + 1)], in_=d[:], func=ACT.Sigmoid)
                     if hf == 1:
                         store(c)

@@ -74,17 +74,18 @@ def tile_classifiermodel_w_kernel(tc, features, roi, conv_w_words, conv_w_scales
                 return cls_pl[4 * g:P, c0:c0 + n]
             return mix_pl[4 * (g - 4):P, c0:c0 + n]
 
-        def spread_bias(r, dst, on_vector):
+        def spread_bias(r, dst, on_vector, by_word=False):
             bp = psum.tile([P, BANK], F32, tag="bank", name="bp%d" % r)
             if r < 12:
                 lhsT = ident_b[:, r:r + 1].to_broadcast([P, P])
             else:
                 lhsT = sel[:, r - 12:r - 11].to_broadcast([P, P])
             nc.tensor.matmul(out=bp[:], lhsT=lhsT, rhs=brow[:], start=True, stop=True)
+            src = bp[:].rearrange("p (q t) -> p t q", t=4) if by_word else bp[:]
             if on_vector:
-                nc.vector.tensor_copy(out=dst, in_=bp[:])
+                nc.vector.tensor_copy(out=dst, in_=src)
             else:
-                nc.scalar.copy(out=dst, in_=bp[:])
+                nc.scalar.copy(out=dst, in_=src)
 
         with tc.tile_pool(name="s1", bufs=1) as s1:
             x_sb = s1.tile([P, C], BF16)
@@ -105,6 +106,18 @@ def tile_classifiermodel_w_kernel(tc, features, roi, conv_w_words, conv_w_scales
             nc.scalar.dma_start(out=brow[0:6, :], in_=conv_b.rearrange("(r c) -> r c", c=BANK))
             nc.scalar.dma_start(out=brow[6:12, :], in_=bbox_b[NP:4 * NP].rearrange("(r c) -> r c", c=BANK))
             nc.scalar.dma_start(out=brow[12:16, :], in_=cls_b.rearrange("(r c) -> r c", c=BANK))
+            for q in range(4):
+                nc.gpsimd.dma_start(out=bbox_pl[32 * q:32 * q + 16, :].bitcast(F32),
+                                  in_=bbox_w_scales[0:4, 4 * q:4 * q + 4, NP:4 * NP].bitcast(F32))
+            for q in range(4):
+                nc.gpsimd.dma_start(out=mix_pl[32 * q + 8:32 * q + 16, :].bitcast(F32),
+                                  in_=bbox_w_scales[4:6, 4 * q:4 * q + 4, NP:4 * NP].bitcast(F32))
+            for q in range(4):
+                nc.gpsimd.dma_start(out=mix_pl[32 * q:32 * q + 8, 0:2 * NP].bitcast(F32),
+                                  in_=cls_w_scales[4:6, 4 * q:4 * q + 4, :].bitcast(F32))
+            for q in range(4):
+                nc.gpsimd.dma_start(out=cls_pl[32 * q:32 * q + 16, :].bitcast(F32),
+                                  in_=cls_w_scales[0:4, 4 * q:4 * q + 4, :].bitcast(F32))
             b_w = []
 
             def load_b(g):
@@ -112,20 +125,8 @@ def tile_classifiermodel_w_kernel(tc, features, roi, conv_w_words, conv_w_scales
                 nc.sync.dma_start(out=w[:].bitcast(I32), in_=words(bbox_w_words[g][:, 4 * NP - NB:4 * NP, :]))
                 b_w.append(w)
 
-            def load_scales(plane, first, scales, g0, g1, n0, n1):
-                for q in range(4):
-                    rows = slice(32 * q + first, 32 * q + first + 4 * (g1 - g0))
-                    nc.sync.dma_start(out=plane[rows, 0:n1 - n0].bitcast(I32),
-                                      in_=scales[g0:g1, 4 * q:4 * q + 4, n0:n1].bitcast(I32))
-
-            load_scales(bbox_pl, 0, bbox_w_scales, 0, 4, NP, 4 * NP)
-            load_b(0)
-            load_scales(mix_pl, 8, bbox_w_scales, 4, 6, NP, 4 * NP)
-            load_b(1)
-            load_scales(mix_pl, 0, cls_w_scales, 4, 6, 0, 2 * NP)
-            load_b(2)
-            load_scales(cls_pl, 0, cls_w_scales, 0, 4, 0, 2 * NP)
-            load_b(3)
+            for g in range(4):
+                load_b(g)
             nc.sync.dma_start(out=roi_sb[:], in_=roi)
 
             x32 = x_sb[:].bitcast(F32)
@@ -140,9 +141,13 @@ def tile_classifiermodel_w_kernel(tc, features, roi, conv_w_words, conv_w_scales
                 nc.vector.tensor_copy(out=fg32[:, 2 * a:2 * a + 2, :, :], in_=xt[:].rearrange("p g u b -> p g b u"))
             nc.vector.quantize_mx(out=fcodes[:].bitcast(FP8X4), scales=fscales[:], in_=fgrouped[:])
 
-            cbias = s1.tile([P, D], BF16)
+            cbias = s1.tile([P, GD, 4, P], BF16)
             for r in range(6):
-                spread_bias(r, cbias[:, BANK * r:BANK * (r + 1)], r % 2 == 0)
+                spread_bias(r, cbias[:, r, :, :], r % 2 == 0, True)
+            for r in range(6, 12):
+                spread_bias(r, bbias[:, BANK * (r - 6):BANK * (r - 5)], r % 2 == 0)
+            for r in range(12, 14):
+                spread_bias(r, dbias[:, BANK * (r - 12):BANK * (r - 11)], r % 2 == 0)
 
             hacc = []
             for j in range(GD):
@@ -159,23 +164,17 @@ def tile_classifiermodel_w_kernel(tc, features, roi, conv_w_words, conv_w_scales
             for g in range(4, GD):
                 load_b(g)
             for j in range(GD):
-                tmp = s1.tile([P, BANK], F32, tag="tmp", bufs=3, name="tmp%d" % j)
-                nc.vector.tensor_tensor(out=tmp[:], in0=hacc[j][:], in1=cbias[:, BANK * j:BANK * (j + 1)],
-                                        op=ALU.add)
                 hperm = s1.tile([P, 4, P], BF16, tag="hperm", bufs=3, name="hperm%d" % j)
-                nc.scalar.activation(out=hperm[:], in_=tmp[:].rearrange("p (q t) -> p t q", t=4), func=ACT.Relu)
+                nc.vector.tensor_tensor(out=hperm[:], in0=hacc[j][:].rearrange("p (q t) -> p t q", t=4),
+                                        in1=cbias[:, j, :, :], op=ALU.add)
                 ht = psum.tile([P, 4, B], BF16, tag="bank", name="ht%d" % j)
                 for t in range(4):
                     nc.tensor.transpose(ht[:, t, :], hperm[:, t, :], ident_b[:])
                 hg = s1.tile([P, B, 4], BF16, tag="hg", bufs=3, name="hg%d" % j, align_bytes=64)
-                nc.vector.tensor_copy(out=hg[:], in_=ht[:].rearrange("p t b -> p b t"))
+                nc.scalar.activation(out=hg[:], in_=ht[:].rearrange("p t b -> p b t"), func=ACT.Relu)
                 nc.vector.quantize_mx(out=hcodes[:, B * j:B * (j + 1)].bitcast(FP8X4),
                                       scales=hscales[:, B * j:B * (j + 1)],
                                       in_=hg[:].rearrange("p b t -> p (b t)"))
-            for r in range(6, 12):
-                spread_bias(r, bbias[:, BANK * (r - 6):BANK * (r - 5)], r % 2 == 0)
-            for r in range(12, 14):
-                spread_bias(r, dbias[:, BANK * (r - 12):BANK * (r - 11)], r % 2 == 0)
 
         def head_pass(acc, g, rhs, rhs_scale, start, stop):
             nc.tensor.matmul_mx(out=acc,
@@ -200,31 +199,44 @@ def tile_classifiermodel_w_kernel(tc, features, roi, conv_w_words, conv_w_scales
                 acc = psum.tile([P, BANK], F32, tag="bank", name="bacc%d" % k)
                 bacc.append(acc)
             for g in range(GD):
-                for k in range(5):
+                for k in (0, 2, 4, 1, 3):
                     head_pass(bacc[k][:], g, b_w[g][:, BANK * k:BANK * (k + 1)],
                               bbox_scale(g, BANK * (k + 1), BANK), g == 0, g == GD - 1)
 
             cls_w = []
-            for g in range(GD - 1):
+            for g in range(4):
                 w = wpool.tile([P, 2 * NP], U32, tag="w12", bufs=8, name="clsw%d" % g, align_bytes=64)
                 nc.sync.dma_start(out=w[:].bitcast(I32), in_=words(cls_w_words[g]))
                 cls_w.append(w)
-            c0_last = wpool.tile([P, NP], U32, tag="tail", bufs=5, name="c0l", align_bytes=64)
-            nc.sync.dma_start(out=c0_last[:].bitcast(I32), in_=words(cls_w_words[GD - 1][:, 0:NP, :]))
-            c1_last = {}
+            cls_last = {}
             for hf in (1, 0):
-                w = wpool.tile([P, BANK], U32, tag="tail", bufs=5, name="c1l%d" % hf, align_bytes=64)
-                nc.sync.dma_start(out=w[:].bitcast(I32),
-                                  in_=words(cls_w_words[GD - 1][:, NP + BANK * hf:NP + BANK * (hf + 1), :]))
-                c1_last[hf] = w
+                for g in range(4, GD):
+                    w = wpool.tile([P, 2, BANK], U32, tag="tail", bufs=6, name="clsl%d_%d" % (hf, g), align_bytes=64)
+                    nc.sync.dma_start(out=w[:].bitcast(I32),
+                                      in_=cls_w_words[g].rearrange("p (s n) t -> p s (n t)", s=2)
+                                      [:, :, 4 * BANK * hf:4 * BANK * (hf + 1)].bitcast(I32))
+                    cls_last[hf, g] = w
             x_w = {}
-            for g0, g1 in ((0, 4), (4, 6)):
-                w = wpool.tile([P, g1 - g0, BANK], U32, tag="tail", bufs=5, name="xw%d" % g0, align_bytes=64)
+            for c in (1, 0):
+                w = wpool.tile([P, GD, CH], U32, tag="tail", bufs=6, name="xw%d" % c, align_bytes=64)
                 nc.sync.dma_start(out=w[:].bitcast(I32),
-                                  in_=bbox_w_words[g0:g1, :, NP:NP + BANK, :]
+                                  in_=bbox_w_words[:, :, NP + CH * c:NP + CH * (c + 1), :]
                                   .rearrange("g p n t -> p g (n t)").bitcast(I32))
-                for g in range(g0, g1):
-                    x_w[g] = w[:, g - g0, :]
+                x_w[c] = w
+
+            obs = []
+            for c in range(4):
+                ob = s2.tile([P, CH, 5], F32, tag="ob", bufs=4, name="ob%d" % c)
+                obs.append(ob)
+
+            def cols(c):
+                return slice(CH * c, CH * (c + 1))
+
+            def lay(c, p0, p1):
+                nc.vector.tensor_copy(out=obs[c][:, :, p0:p1], in_=planes[:, p0:p1, cols(c)].rearrange("p c n -> p n c"))
+
+            def store(c):
+                nc.sync.dma_start(out=out[:, cols(c), :], in_=obs[c][:])
 
             def x_out(acc, sl, n):
                 tx = s2.tile([P, n], F32, tag="tx", bufs=2, name="tx%d" % sl.start)
@@ -232,15 +244,9 @@ def tile_classifiermodel_w_kernel(tc, features, roi, conv_w_words, conv_w_scales
                                                op0=ALU.mult, op1=ALU.mult)
                 nc.vector.tensor_tensor(out=planes[:, 0, sl], in0=planes[:, 0, sl], in1=tx[:], op=ALU.subtract)
 
-            def store(c):
-                sl = slice(CH * c, CH * (c + 1))
-                ob = s2.tile([P, CH, 5], F32, tag="ob", bufs=4, name="ob%d" % c)
-                nc.vector.tensor_copy(out=ob[:], in_=planes[:, :, sl].rearrange("p c n -> p n c"))
-                nc.sync.dma_start(out=out[:, sl, :], in_=ob[:])
-
             x_out(bacc[0][:], slice(BANK, NP), BANK)
             e = None
-            for j in range(4):
+            for j in (1, 3, 0, 2):
                 comp = 2 + j // 2
                 sl = slice(BANK * (j % 2), BANK * (j % 2 + 1))
                 u = s2.tile([P, BANK], F32, tag="u", bufs=2, name="u%d" % j)
@@ -253,48 +259,49 @@ def tile_classifiermodel_w_kernel(tc, features, roi, conv_w_words, conv_w_scales
                                                op0=ALU.mult, op1=ALU.mult)
             warm = s2.tile([P, 1], F32)
             nc.scalar.activation(out=warm[:], in_=e[:, 0:1], func=ACT.Sigmoid)
+            for c in (2, 3):
+                lay(c, 0, 4)
+            lay(1, 1, 4)
 
             c0acc = []
             c1acc = []
             for hf in range(2):
                 acc = psum.tile([P, BANK], F32, tag="bank", name="c0acc%d" % hf)
                 c0acc.append(acc)
-            for hf in range(2):
                 acc = psum.tile([P, BANK], F32, tag="bank", name="c1acc%d" % hf)
                 c1acc.append(acc)
-            for g in range(GD - 1):
-                for hf in range(2):
+            for g in range(4):
+                for hf in (1, 0):
                     head_pass(c0acc[hf][:], g, cls_w[g][:, BANK * hf:BANK * (hf + 1)],
                               cls_scale(g, BANK * hf, BANK), g == 0, False)
-                for hf in range(2):
                     head_pass(c1acc[hf][:], g, cls_w[g][:, NP + BANK * hf:NP + BANK * (hf + 1)],
                               cls_scale(g, NP + BANK * hf, BANK), g == 0, False)
             e0 = s2.tile([P, NP], F32)
             for hf in (1, 0):
                 sl = slice(BANK * hf, BANK * (hf + 1))
-                head_pass(c0acc[hf][:], GD - 1, c0_last[:, sl], cls_scale(GD - 1, BANK * hf, BANK), False, True)
+                for g in range(4, GD):
+                    head_pass(c0acc[hf][:], g, cls_last[hf, g][:, 0, :], cls_scale(g, BANK * hf, BANK),
+                              False, g == GD - 1)
+                    head_pass(c1acc[hf][:], g, cls_last[hf, g][:, 1, :], cls_scale(g, NP + BANK * hf, BANK),
+                              False, g == GD - 1)
                 nc.vector.tensor_tensor(out=e0[:, sl], in0=c0acc[hf][:], in1=dbias[:, sl], op=ALU.subtract)
-            for hf in (1, 0):
-                head_pass(c1acc[hf][:], GD - 1, c1_last[hf][:], cls_scale(GD - 1, NP + BANK * hf, BANK), False, True)
-                for c in (2 * hf, 2 * hf + 1):
+                for c in ((2, 3) if hf == 1 else (1, 0)):
                     off = CH * (c - 2 * hf)
                     d = s2.tile([P, CH], F32, tag="d", bufs=2, name="d%d" % c)
-                    nc.vector.tensor_tensor(out=d[:], in0=c1acc[hf][:, off:off + CH],
-                                            in1=e0[:, CH * c:CH * (c + 1)], op=ALU.subtract)
-                    nc.scalar.activation(out=planes[:, 4, CH * c:CH * (c + 1)], in_=d[:], func=ACT.Sigmoid)
+                    nc.vector.tensor_tensor(out=d[:], in0=c1acc[hf][:, off:off + CH], in1=e0[:, cols(c)],
+                                            op=ALU.subtract)
+                    if c == 1:
+                        nc.scalar.activation(out=obs[c][:, :, 4], in_=d[:], func=ACT.Sigmoid)
+                    else:
+                        nc.scalar.activation(out=planes[:, 4, cols(c)], in_=d[:], func=ACT.Sigmoid)
                     if hf == 1:
+                        lay(c, 4, 5)
                         store(c)
 
-            xacc = []
-            for c in range(2):
+            for c in (1, 0):
                 acc = psum.tile([P, CH], F32, tag="bank", name="xacc%d" % c)
-                xacc.append(acc)
-            for g in range(4):
-                for c in range(2):
-                    head_pass(xacc[c][:], g, x_w[g][:, CH * c:CH * (c + 1)], bbox_scale(g, CH * c, CH), g == 0, False)
-            for c in range(2):
-                for g in range(4, GD):
-                    head_pass(xacc[c][:], g, x_w[g][:, CH * c:CH * (c + 1)], bbox_scale(g, CH * c, CH),
-                              False, g == GD - 1)
-                x_out(xacc[c][:], slice(CH * c, CH * (c + 1)), CH)
+                for g in range(GD):
+                    head_pass(acc[:], g, x_w[c][:, g, :], bbox_scale(g, CH * c, CH), g == 0, g == GD - 1)
+                x_out(acc[:], cols(c), CH)
+                lay(c, 0, 1 if c == 1 else 5)
                 store(c)

@@ -211,18 +211,20 @@ def tile_classifiermodel_w_kernel(tc, features, roi, conv_w_words, conv_w_scales
             cls_last = {}
             for hf in (1, 0):
                 for g in range(4, GD):
-                    w = wpool.tile([P, 2, BANK], U32, tag="tail", bufs=6, name="clsl%d_%d" % (hf, g), align_bytes=64)
+                    w = wpool.tile([P, 2, BANK], U32, tag="tail", bufs=8, name="clsl%d_%d" % (hf, g), align_bytes=64)
                     nc.sync.dma_start(out=w[:].bitcast(I32),
                                       in_=cls_w_words[g].rearrange("p (s n) t -> p s (n t)", s=2)
                                       [:, :, 4 * BANK * hf:4 * BANK * (hf + 1)].bitcast(I32))
                     cls_last[hf, g] = w
             x_w = {}
             for c in (1, 0):
-                w = wpool.tile([P, GD, CH], U32, tag="tail", bufs=6, name="xw%d" % c, align_bytes=64)
-                nc.sync.dma_start(out=w[:].bitcast(I32),
-                                  in_=bbox_w_words[:, :, NP + CH * c:NP + CH * (c + 1), :]
-                                  .rearrange("g p n t -> p g (n t)").bitcast(I32))
-                x_w[c] = w
+                for g0, g1 in ((0, 4), (4, 6)):
+                    w = wpool.tile([P, g1 - g0, CH], U32, tag="tail", bufs=8, name="xw%d_%d" % (c, g0), align_bytes=64)
+                    nc.sync.dma_start(out=w[:].bitcast(I32),
+                                      in_=bbox_w_words[g0:g1, :, NP + CH * c:NP + CH * (c + 1), :]
+                                      .rearrange("g p n t -> p g (n t)").bitcast(I32))
+                    for g in range(g0, g1):
+                        x_w[c, g] = w[:, g - g0, :]
 
             obs = []
             for c in range(4):
@@ -276,32 +278,40 @@ def tile_classifiermodel_w_kernel(tc, features, roi, conv_w_words, conv_w_scales
                               cls_scale(g, BANK * hf, BANK), g == 0, False)
                     head_pass(c1acc[hf][:], g, cls_w[g][:, NP + BANK * hf:NP + BANK * (hf + 1)],
                               cls_scale(g, NP + BANK * hf, BANK), g == 0, False)
-            e0 = s2.tile([P, NP], F32)
+
+            def objectness(c):
+                hf, off = divmod(CH * c, BANK)
+                e0 = s2.tile([P, CH], F32, tag="e0", bufs=2, name="e0_%d" % c)
+                nc.vector.tensor_tensor(out=e0[:], in0=c0acc[hf][:, off:off + CH], in1=dbias[:, cols(c)], op=ALU.subtract)
+                d = s2.tile([P, CH], F32, tag="d", bufs=2, name="d%d" % c)
+                nc.vector.tensor_tensor(out=d[:], in0=c1acc[hf][:, off:off + CH], in1=e0[:], op=ALU.subtract)
+                dst = obs[c][:, :, 4] if c == 1 else planes[:, 4, cols(c)]
+                nc.scalar.activation(out=dst, in_=d[:], func=ACT.Sigmoid)
+
             for hf in (1, 0):
-                sl = slice(BANK * hf, BANK * (hf + 1))
                 for g in range(4, GD):
                     head_pass(c0acc[hf][:], g, cls_last[hf, g][:, 0, :], cls_scale(g, BANK * hf, BANK),
                               False, g == GD - 1)
                     head_pass(c1acc[hf][:], g, cls_last[hf, g][:, 1, :], cls_scale(g, NP + BANK * hf, BANK),
                               False, g == GD - 1)
-                nc.vector.tensor_tensor(out=e0[:, sl], in0=c0acc[hf][:], in1=dbias[:, sl], op=ALU.subtract)
-                for c in ((2, 3) if hf == 1 else (1, 0)):
-                    off = CH * (c - 2 * hf)
-                    d = s2.tile([P, CH], F32, tag="d", bufs=2, name="d%d" % c)
-                    nc.vector.tensor_tensor(out=d[:], in0=c1acc[hf][:, off:off + CH], in1=e0[:, cols(c)],
-                                            op=ALU.subtract)
-                    if c == 1:
-                        nc.scalar.activation(out=obs[c][:, :, 4], in_=d[:], func=ACT.Sigmoid)
-                    else:
-                        nc.scalar.activation(out=planes[:, 4, cols(c)], in_=d[:], func=ACT.Sigmoid)
-                    if hf == 1:
+                if hf == 1:
+                    for c in (2, 3):
+                        objectness(c)
                         lay(c, 4, 5)
                         store(c)
 
             for c in (1, 0):
+                objectness(c)
                 acc = psum.tile([P, CH], F32, tag="bank", name="xacc%d" % c)
                 for g in range(GD):
-                    head_pass(acc[:], g, x_w[c][:, g, :], bbox_scale(g, CH * c, CH), g == 0, g == GD - 1)
-                x_out(acc[:], cols(c), CH)
-                lay(c, 0, 1 if c == 1 else 5)
-                store(c)
+                    head_pass(acc[:], g, x_w[c, g], bbox_scale(g, CH * c, CH), g == 0, g == GD - 1)
+                if c == 1:
+                    x_out(acc[:], cols(c), CH)
+                    lay(c, 0, 1)
+                    store(c)
+                else:
+                    for o in range(0, CH, P):
+                        sl = slice(o, o + P)
+                        x_out(acc[:, sl], sl, P)
+                        nc.vector.tensor_copy(out=obs[0][:, sl, :], in_=planes[:, :, sl].rearrange("p c n -> p n c"))
+                        nc.sync.dma_start(out=out[:, sl, :], in_=obs[0][:, sl, :])

@@ -99,8 +99,8 @@ def tile_classifiermodel_w_kernel(tc, features, roi, conv_w_words, conv_w_scales
 
             load_conv(0)
             for q in range(4):
-                nc.sync.dma_start(out=conv_pl[32 * q:32 * q + 16, :].bitcast(I32),
-                                  in_=conv_w_scales[:, 4 * q:4 * q + 4, :].bitcast(I32))
+                nc.gpsimd.dma_start(out=conv_pl[32 * q:32 * q + 16, :].bitcast(F32),
+                                    in_=conv_w_scales[:, 4 * q:4 * q + 4, :].bitcast(F32))
             for g in range(1, GC):
                 load_conv(g)
             nc.scalar.dma_start(out=brow[0:6, :], in_=conv_b.rearrange("(r c) -> r c", c=BANK))
@@ -279,12 +279,18 @@ def tile_classifiermodel_w_kernel(tc, features, roi, conv_w_words, conv_w_scales
                     head_pass(c1acc[hf][:], g, cls_w[g][:, NP + BANK * hf:NP + BANK * (hf + 1)],
                               cls_scale(g, NP + BANK * hf, BANK), g == 0, False)
 
-            def objectness(c):
+            e0s = {}
+
+            def base(c):
                 hf, off = divmod(CH * c, BANK)
                 e0 = s2.tile([P, CH], F32, tag="e0", bufs=2, name="e0_%d" % c)
                 nc.vector.tensor_tensor(out=e0[:], in0=c0acc[hf][:, off:off + CH], in1=dbias[:, cols(c)], op=ALU.subtract)
+                e0s[c] = e0
+
+            def objectness(c):
+                hf, off = divmod(CH * c, BANK)
                 d = s2.tile([P, CH], F32, tag="d", bufs=2, name="d%d" % c)
-                nc.vector.tensor_tensor(out=d[:], in0=c1acc[hf][:, off:off + CH], in1=e0[:], op=ALU.subtract)
+                nc.vector.tensor_tensor(out=d[:], in0=c1acc[hf][:, off:off + CH], in1=e0s[c][:], op=ALU.subtract)
                 dst = obs[c][:, :, 4] if c == 1 else planes[:, 4, cols(c)]
                 nc.scalar.activation(out=dst, in_=d[:], func=ACT.Sigmoid)
 
@@ -296,22 +302,34 @@ def tile_classifiermodel_w_kernel(tc, features, roi, conv_w_words, conv_w_scales
                               False, g == GD - 1)
                 if hf == 1:
                     for c in (2, 3):
+                        base(c)
+                    for c in (2, 3):
                         objectness(c)
+                    for c in (2, 3):
                         lay(c, 4, 5)
                         store(c)
 
+            for c in (1, 0):
+                base(c)
             for c in (1, 0):
                 objectness(c)
                 acc = psum.tile([P, CH], F32, tag="bank", name="xacc%d" % c)
                 for g in range(GD):
                     head_pass(acc[:], g, x_w[c, g], bbox_scale(g, CH * c, CH), g == 0, g == GD - 1)
+                halves = [slice(CH * c + o, CH * c + o + P) for o in range(0, CH, P)]
+                txs = []
+                for i in range(2):
+                    tx = s2.tile([P, P], F32, tag="txh", bufs=4, name="txh%d_%d" % (c, i))
+                    nc.vector.scalar_tensor_tensor(out=tx[:], in0=acc[:, P * i:P * (i + 1)], scalar=16.0,
+                                                   in1=roi_sb[:, halves[i], 3], op0=ALU.mult, op1=ALU.mult)
+                    txs.append(tx)
+                for i in range(2):
+                    nc.vector.tensor_tensor(out=planes[:, 0, halves[i]], in0=planes[:, 0, halves[i]], in1=txs[i][:],
+                                            op=ALU.subtract)
                 if c == 1:
-                    x_out(acc[:], cols(c), CH)
                     lay(c, 0, 1)
                     store(c)
                 else:
-                    for o in range(0, CH, P):
-                        sl = slice(o, o + P)
-                        x_out(acc[:, sl], sl, P)
+                    for sl in halves:
                         nc.vector.tensor_copy(out=obs[0][:, sl, :], in_=planes[:, :, sl].rearrange("p c n -> p n c"))
                         nc.sync.dma_start(out=out[:, sl, :], in_=obs[0][:, sl, :])

@@ -208,18 +208,20 @@ def tile_classifiermodel_w_kernel(tc, features, roi, conv_w_words, conv_w_scales
                 w = wpool.tile([P, 2 * NP], U32, tag="w12", bufs=8, name="clsw%d" % g, align_bytes=64)
                 nc.sync.dma_start(out=w[:].bitcast(I32), in_=words(cls_w_words[g]))
                 cls_w.append(w)
-            cls_last = {}
+            c0_last = wpool.tile([P, 2, NP], U32, tag="c0l", bufs=1, name="c0l", align_bytes=64)
+            nc.sync.dma_start(out=c0_last[:].bitcast(I32),
+                              in_=cls_w_words[4:6, :, 0:NP, :].rearrange("g p n t -> p g (n t)").bitcast(I32))
+            c1_last = {}
             for hf in (1, 0):
-                for g in range(4, GD):
-                    w = wpool.tile([P, 2, BANK], U32, tag="tail", bufs=8, name="clsl%d_%d" % (hf, g), align_bytes=64)
-                    nc.sync.dma_start(out=w[:].bitcast(I32),
-                                      in_=cls_w_words[g].rearrange("p (s n) t -> p s (n t)", s=2)
-                                      [:, :, 4 * BANK * hf:4 * BANK * (hf + 1)].bitcast(I32))
-                    cls_last[hf, g] = w
+                n0 = NP + BANK * hf
+                w = wpool.tile([P, 2, BANK], U32, tag="tail", bufs=6, name="c1l%d" % hf, align_bytes=64)
+                nc.sync.dma_start(out=w[:].bitcast(I32),
+                                  in_=cls_w_words[4:6, :, n0:n0 + BANK, :].rearrange("g p n t -> p g (n t)").bitcast(I32))
+                c1_last[hf] = w
             x_w = {}
             for c in (1, 0):
                 for g0, g1 in ((0, 4), (4, 6)):
-                    w = wpool.tile([P, g1 - g0, CH], U32, tag="tail", bufs=8, name="xw%d_%d" % (c, g0), align_bytes=64)
+                    w = wpool.tile([P, g1 - g0, CH], U32, tag="tail", bufs=6, name="xw%d_%d" % (c, g0), align_bytes=64)
                     nc.sync.dma_start(out=w[:].bitcast(I32),
                                       in_=bbox_w_words[g0:g1, :, NP + CH * c:NP + CH * (c + 1), :]
                                       .rearrange("g p n t -> p g (n t)").bitcast(I32))
@@ -233,6 +235,9 @@ def tile_classifiermodel_w_kernel(tc, features, roi, conv_w_words, conv_w_scales
 
             def cols(c):
                 return slice(CH * c, CH * (c + 1))
+
+            def lay_on_scalar(c, p0, p1):
+                nc.scalar.copy(out=obs[c][:, :, p0:p1], in_=planes[:, p0:p1, cols(c)].rearrange("p c n -> p n c"))
 
             def lay(c, p0, p1):
                 nc.vector.tensor_copy(out=obs[c][:, :, p0:p1], in_=planes[:, p0:p1, cols(c)].rearrange("p c n -> p n c"))
@@ -263,7 +268,7 @@ def tile_classifiermodel_w_kernel(tc, features, roi, conv_w_words, conv_w_scales
             nc.scalar.activation(out=warm[:], in_=e[:, 0:1], func=ACT.Sigmoid)
             for c in (2, 3):
                 lay(c, 0, 4)
-            lay(1, 1, 4)
+            lay_on_scalar(1, 1, 4)
 
             c0acc = []
             c1acc = []
@@ -283,26 +288,28 @@ def tile_classifiermodel_w_kernel(tc, features, roi, conv_w_words, conv_w_scales
 
             def base(c):
                 hf, off = divmod(CH * c, BANK)
-                e0 = s2.tile([P, CH], F32, tag="e0", bufs=2, name="e0_%d" % c)
+                e0 = s2.tile([P, CH], F32, tag="e0", bufs=4, name="e0_%d" % c)
                 nc.vector.tensor_tensor(out=e0[:], in0=c0acc[hf][:, off:off + CH], in1=dbias[:, cols(c)], op=ALU.subtract)
                 e0s[c] = e0
 
             def objectness(c):
                 hf, off = divmod(CH * c, BANK)
-                d = s2.tile([P, CH], F32, tag="d", bufs=2, name="d%d" % c)
+                d = s2.tile([P, CH], F32, tag="d", bufs=4, name="d%d" % c)
                 nc.vector.tensor_tensor(out=d[:], in0=c1acc[hf][:, off:off + CH], in1=e0s[c][:], op=ALU.subtract)
                 dst = obs[c][:, :, 4] if c == 1 else planes[:, 4, cols(c)]
                 nc.scalar.activation(out=dst, in_=d[:], func=ACT.Sigmoid)
 
             for hf in (1, 0):
                 for g in range(4, GD):
-                    head_pass(c0acc[hf][:], g, cls_last[hf, g][:, 0, :], cls_scale(g, BANK * hf, BANK),
-                              False, g == GD - 1)
-                    head_pass(c1acc[hf][:], g, cls_last[hf, g][:, 1, :], cls_scale(g, NP + BANK * hf, BANK),
+                    head_pass(c0acc[hf][:], g, c0_last[:, g - 4, BANK * hf:BANK * (hf + 1)],
+                              cls_scale(g, BANK * hf, BANK), False, g == GD - 1)
+            for c in (2, 3, 1, 0):
+                base(c)
+            for hf in (1, 0):
+                for g in range(4, GD):
+                    head_pass(c1acc[hf][:], g, c1_last[hf][:, g - 4, :], cls_scale(g, NP + BANK * hf, BANK),
                               False, g == GD - 1)
                 if hf == 1:
-                    for c in (2, 3):
-                        base(c)
                     for c in (2, 3):
                         objectness(c)
                     for c in (2, 3):
@@ -310,9 +317,9 @@ def tile_classifiermodel_w_kernel(tc, features, roi, conv_w_words, conv_w_scales
                         store(c)
 
             for c in (1, 0):
-                base(c)
-            for c in (1, 0):
                 objectness(c)
+            lay_on_scalar(0, 1, 5)
+            for c in (1, 0):
                 acc = psum.tile([P, CH], F32, tag="bank", name="xacc%d" % c)
                 for g in range(GD):
                     head_pass(acc[:], g, x_w[c, g], bbox_scale(g, CH * c, CH), g == 0, g == GD - 1)
@@ -331,5 +338,5 @@ def tile_classifiermodel_w_kernel(tc, features, roi, conv_w_words, conv_w_scales
                     store(c)
                 else:
                     for sl in halves:
-                        nc.vector.tensor_copy(out=obs[0][:, sl, :], in_=planes[:, :, sl].rearrange("p c n -> p n c"))
+                        nc.vector.tensor_copy(out=obs[0][:, sl, 0], in_=planes[:, 0, sl])
                         nc.sync.dma_start(out=out[:, sl, :], in_=obs[0][:, sl, :])

@@ -60,6 +60,8 @@ def tile_classifiermodel_w_kernel(tc, features, roi, conv_w_words, conv_w_scales
         fscales = const.tile([P, GC * B], U8, align_bytes=64)
         hcodes = const.tile([P, GD * B], U32, align_bytes=64)
         hscales = const.tile([P, GD * B], U8, align_bytes=64)
+        ncodes = const.tile([P, GD * B], U32, align_bytes=64)
+        nscales = const.tile([P, GD * B], U8, align_bytes=64)
         bbias = const.tile([P, 3 * NP], BF16)
         dbias = const.tile([P, NP], F32)
         roi_sb = const.tile([P, NP, 4], BF16)
@@ -163,6 +165,7 @@ def tile_classifiermodel_w_kernel(tc, features, roi, conv_w_words, conv_w_scales
                                         start=(g == 0), stop=(g == GC - 1))
             for g in range(4, GD):
                 load_b(g)
+            hgs = []
             for j in range(GD):
                 hperm = s1.tile([P, 4, P], BF16, tag="hperm", bufs=3, name="hperm%d" % j)
                 nc.vector.tensor_tensor(out=hperm[:], in0=hacc[j][:].rearrange("p (q t) -> p t q", t=4),
@@ -170,16 +173,25 @@ def tile_classifiermodel_w_kernel(tc, features, roi, conv_w_words, conv_w_scales
                 ht = psum.tile([P, 4, B], BF16, tag="bank", name="ht%d" % j)
                 for t in range(4):
                     nc.tensor.transpose(ht[:, t, :], hperm[:, t, :], ident_b[:])
-                hg = s1.tile([P, B, 4], BF16, tag="hg", bufs=3, name="hg%d" % j, align_bytes=64)
+                hg = s1.tile([P, B, 4], BF16, tag="hg", bufs=6, name="hg%d" % j, align_bytes=64)
+                hgs.append(hg)
                 nc.scalar.activation(out=hg[:], in_=ht[:].rearrange("p t b -> p b t"), func=ACT.Relu)
                 nc.vector.quantize_mx(out=hcodes[:, B * j:B * (j + 1)].bitcast(FP8X4),
                                       scales=hscales[:, B * j:B * (j + 1)],
                                       in_=hg[:].rearrange("p b t -> p (b t)"))
+            for j in range(GD):
+                hgn = s1.tile([P, B, 4], BF16, tag="hgn", bufs=3, name="hgn%d" % j, align_bytes=64)
+                nc.scalar.activation(out=hgn[:], in_=hgs[j][:], func=ACT.Copy, scale=-1.0)
+                nc.vector.quantize_mx(out=ncodes[:, B * j:B * (j + 1)].bitcast(FP8X4),
+                                      scales=nscales[:, B * j:B * (j + 1)],
+                                      in_=hgn[:].rearrange("p b t -> p (b t)"))
 
-        def head_pass(acc, g, rhs, rhs_scale, start, stop):
+        def head_pass(acc, g, rhs, rhs_scale, start, stop, negated=False):
+            codes = ncodes if negated else hcodes
+            scales = nscales if negated else hscales
             nc.tensor.matmul_mx(out=acc,
-                                lhsT=hcodes[:, B * g:B * (g + 1)].bitcast(FP8X4),
-                                lhsT_scale=hscales[:, B * g:B * (g + 1)],
+                                lhsT=codes[:, B * g:B * (g + 1)].bitcast(FP8X4),
+                                lhsT_scale=scales[:, B * g:B * (g + 1)],
                                 rhs=rhs.bitcast(FP8X4), rhs_scale=rhs_scale,
                                 start=start, stop=stop)
 
@@ -208,20 +220,19 @@ def tile_classifiermodel_w_kernel(tc, features, roi, conv_w_words, conv_w_scales
                 w = wpool.tile([P, 2 * NP], U32, tag="w12", bufs=8, name="clsw%d" % g, align_bytes=64)
                 nc.sync.dma_start(out=w[:].bitcast(I32), in_=words(cls_w_words[g]))
                 cls_w.append(w)
-            c0_last = wpool.tile([P, 2, NP], U32, tag="c0l", bufs=1, name="c0l", align_bytes=64)
-            nc.sync.dma_start(out=c0_last[:].bitcast(I32),
-                              in_=cls_w_words[4:6, :, 0:NP, :].rearrange("g p n t -> p g (n t)").bitcast(I32))
-            c1_last = {}
+            cls_last = {}
             for hf in (1, 0):
-                n0 = NP + BANK * hf
-                w = wpool.tile([P, 2, BANK], U32, tag="tail", bufs=6, name="c1l%d" % hf, align_bytes=64)
-                nc.sync.dma_start(out=w[:].bitcast(I32),
-                                  in_=cls_w_words[4:6, :, n0:n0 + BANK, :].rearrange("g p n t -> p g (n t)").bitcast(I32))
-                c1_last[hf] = w
+                for s in range(2):
+                    n0 = NP * s + BANK * hf
+                    w = wpool.tile([P, 2, BANK], U32, tag="tail", bufs=8, name="clsl%d_%d" % (hf, s), align_bytes=64)
+                    nc.sync.dma_start(out=w[:].bitcast(I32),
+                                      in_=cls_w_words[4:6, :, n0:n0 + BANK, :]
+                                      .rearrange("g p n t -> p g (n t)").bitcast(I32))
+                    cls_last[hf, s] = w
             x_w = {}
             for c in (1, 0):
                 for g0, g1 in ((0, 4), (4, 6)):
-                    w = wpool.tile([P, g1 - g0, CH], U32, tag="tail", bufs=6, name="xw%d_%d" % (c, g0), align_bytes=64)
+                    w = wpool.tile([P, g1 - g0, CH], U32, tag="tail", bufs=8, name="xw%d_%d" % (c, g0), align_bytes=64)
                     nc.sync.dma_start(out=w[:].bitcast(I32),
                                       in_=bbox_w_words[g0:g1, :, NP + CH * c:NP + CH * (c + 1), :]
                                       .rearrange("g p n t -> p g (n t)").bitcast(I32))
@@ -236,14 +247,9 @@ def tile_classifiermodel_w_kernel(tc, features, roi, conv_w_words, conv_w_scales
             def cols(c):
                 return slice(CH * c, CH * (c + 1))
 
-            def lay_on_scalar(c, p0, p1):
-                nc.scalar.copy(out=obs[c][:, :, p0:p1], in_=planes[:, p0:p1, cols(c)].rearrange("p c n -> p n c"))
-
-            def lay(c, p0, p1):
-                nc.vector.tensor_copy(out=obs[c][:, :, p0:p1], in_=planes[:, p0:p1, cols(c)].rearrange("p c n -> p n c"))
-
-            def store(c):
-                nc.sync.dma_start(out=out[:, cols(c), :], in_=obs[c][:])
+            def lay(copy, c, o0, o1, p0, p1):
+                copy(out=obs[c][:, o0:o1, p0:p1],
+                     in_=planes[:, p0:p1, CH * c + o0:CH * c + o1].rearrange("p c n -> p n c"))
 
             def x_out(acc, sl, n):
                 tx = s2.tile([P, n], F32, tag="tx", bufs=2, name="tx%d" % sl.start)
@@ -266,59 +272,47 @@ def tile_classifiermodel_w_kernel(tc, features, roi, conv_w_words, conv_w_scales
                                                op0=ALU.mult, op1=ALU.mult)
             warm = s2.tile([P, 1], F32)
             nc.scalar.activation(out=warm[:], in_=e[:, 0:1], func=ACT.Sigmoid)
-            for c in (2, 3):
-                lay(c, 0, 4)
-            lay_on_scalar(1, 1, 4)
 
-            c0acc = []
-            c1acc = []
+            dacc = []
             for hf in range(2):
-                acc = psum.tile([P, BANK], F32, tag="bank", name="c0acc%d" % hf)
-                c0acc.append(acc)
-                acc = psum.tile([P, BANK], F32, tag="bank", name="c1acc%d" % hf)
-                c1acc.append(acc)
+                acc = psum.tile([P, BANK], F32, tag="bank", name="dacc%d" % hf)
+                dacc.append(acc)
             for g in range(4):
                 for hf in (1, 0):
-                    head_pass(c0acc[hf][:], g, cls_w[g][:, BANK * hf:BANK * (hf + 1)],
-                              cls_scale(g, BANK * hf, BANK), g == 0, False)
-                    head_pass(c1acc[hf][:], g, cls_w[g][:, NP + BANK * hf:NP + BANK * (hf + 1)],
+                    head_pass(dacc[hf][:], g, cls_w[g][:, NP + BANK * hf:NP + BANK * (hf + 1)],
                               cls_scale(g, NP + BANK * hf, BANK), g == 0, False)
+                for hf in (1, 0):
+                    head_pass(dacc[hf][:], g, cls_w[g][:, BANK * hf:BANK * (hf + 1)],
+                              cls_scale(g, BANK * hf, BANK), False, False, negated=True)
 
-            e0s = {}
-
-            def base(c):
+            def objectness(c, o0, o1):
                 hf, off = divmod(CH * c, BANK)
-                e0 = s2.tile([P, CH], F32, tag="e0", bufs=4, name="e0_%d" % c)
-                nc.vector.tensor_tensor(out=e0[:], in0=c0acc[hf][:, off:off + CH], in1=dbias[:, cols(c)], op=ALU.subtract)
-                e0s[c] = e0
-
-            def objectness(c):
-                hf, off = divmod(CH * c, BANK)
-                d = s2.tile([P, CH], F32, tag="d", bufs=4, name="d%d" % c)
-                nc.vector.tensor_tensor(out=d[:], in0=c1acc[hf][:, off:off + CH], in1=e0s[c][:], op=ALU.subtract)
-                dst = obs[c][:, :, 4] if c == 1 else planes[:, 4, cols(c)]
+                sl = slice(CH * c + o0, CH * c + o1)
+                d = s2.tile([P, o1 - o0], F32, tag="d", bufs=4, name="d%d" % sl.start)
+                nc.vector.tensor_tensor(out=d[:], in0=dacc[hf][:, off + o0:off + o1], in1=dbias[:, sl], op=ALU.add)
+                dst = obs[c][:, :, 4] if c == 1 else planes[:, 4, sl]
                 nc.scalar.activation(out=dst, in_=d[:], func=ACT.Sigmoid)
 
+            def store_part(c, o0, o1):
+                nc.sync.dma_start(out=out[:, CH * c + o0:CH * c + o1, :], in_=obs[c][:, o0:o1, :])
+
             for hf in (1, 0):
-                for g in range(4, GD):
-                    head_pass(c0acc[hf][:], g, c0_last[:, g - 4, BANK * hf:BANK * (hf + 1)],
-                              cls_scale(g, BANK * hf, BANK), False, g == GD - 1)
-            for c in (2, 3, 1, 0):
-                base(c)
-            for hf in (1, 0):
-                for g in range(4, GD):
-                    head_pass(c1acc[hf][:], g, c1_last[hf][:, g - 4, :], cls_scale(g, NP + BANK * hf, BANK),
-                              False, g == GD - 1)
+                for s in range(2):
+                    for g in range(4, GD):
+                        head_pass(dacc[hf][:], g, cls_last[hf, s][:, g - 4, :], cls_scale(g, NP * s + BANK * hf, BANK),
+                                  False, s == 1 and g == GD - 1, negated=(s == 0))
                 if hf == 1:
-                    for c in (2, 3):
-                        objectness(c)
-                    for c in (2, 3):
-                        lay(c, 4, 5)
-                        store(c)
+                    parts = ((2, 0, P), (2, P, CH), (3, 0, CH))
+                    for part in parts:
+                        objectness(*part)
+                    for part in parts:
+                        lay(nc.vector.tensor_copy, *part, 0, 5)
+                        store_part(*part)
+            lay(nc.scalar.copy, 1, 0, CH, 1, 4)
 
             for c in (1, 0):
-                objectness(c)
-            lay_on_scalar(0, 1, 5)
+                objectness(c, 0, CH)
+            lay(nc.scalar.copy, 0, 0, P, 1, 5)
             for c in (1, 0):
                 acc = psum.tile([P, CH], F32, tag="bank", name="xacc%d" % c)
                 for g in range(GD):
@@ -333,10 +327,6 @@ def tile_classifiermodel_w_kernel(tc, features, roi, conv_w_words, conv_w_scales
                 for i in range(2):
                     nc.vector.tensor_tensor(out=planes[:, 0, halves[i]], in0=planes[:, 0, halves[i]], in1=txs[i][:],
                                             op=ALU.subtract)
-                if c == 1:
-                    lay(c, 0, 1)
-                    store(c)
-                else:
-                    for sl in halves:
-                        nc.vector.tensor_copy(out=obs[0][:, sl, 0], in_=planes[:, 0, sl])
-                        nc.sync.dma_start(out=out[:, sl, :], in_=obs[0][:, sl, :])
+                for o in range(0, CH, P):
+                    lay(nc.vector.tensor_copy, c, o, o + P, 0, 5 if c == 0 and o == P else 1)
+                    store_part(c, o, o + P)

from contextlib import ExitStack

import concourse.mybir as mybir
from concourse.masks import make_identity

F32 = mybir.dt.float32
BF16 = mybir.dt.bfloat16
I32 = mybir.dt.int32
U32 = mybir.dt.uint32
U8 = mybir.dt.uint8
FP8X4 = mybir.dt.float8_e4m3fn_x4
ALU = mybir.AluOpType
ACT = mybir.ActivationFunctionType

P = 128
B = 128
C = 2048
D = 3072
NP = 1024
GC = C // 512
GD = D // 512
BANK = 512
NB = 5 * BANK
CH = 256

FLOPS = 2 * B * (C * D + D * 2 * NP + D * 3 * NP)
BYTES = (B * C * 2 + B * NP * 4 * 2 + C * D + C * D // 32 + D * 2 + D * 2 * NP + D * 2 * NP // 32 + 2 * NP * 2
         + D * 3 * NP + D * 3 * NP // 32 + 3 * NP * 2 + B * NP * 5 * 4)


def tile_classifiermodel_w_kernel(tc, features, roi, conv_w_words, conv_w_scales, conv_b,
                                             cls_w_words, cls_w_scales, cls_b,
                                             bbox_w_words, bbox_w_scales, bbox_b, out):
    nc = tc.nc

    def words(ap):
        return ap.rearrange("p n t -> p (n t)").bitcast(I32)

    with ExitStack() as ctx:
        const = ctx.enter_context(tc.tile_pool(name="const", bufs=1))
        wpool = ctx.enter_context(tc.tile_pool(name="weights", bufs=1))
        psum = ctx.enter_context(tc.psum_pool(name="psum", bufs=8))

        brow = const.tile([P, BANK], BF16)
        nc.vector.memset(brow[:], 0.0)
        conv_pl = const.tile([P, D], U8, align_bytes=64)
        bbox_pl = const.tile([P, 3 * NP], U8, align_bytes=64)
        cls_pl = const.tile([P, 2 * NP], U8, align_bytes=64)
        mix_pl = const.tile([P, 3 * NP], U8, align_bytes=64)
        for pl in (conv_pl, bbox_pl, mix_pl, cls_pl):
            nc.vector.memset(pl[:].bitcast(I32), 0)
        ident_f = const.tile([P, P], F32)
        make_identity(nc, ident_f[:])
        ident_b = const.tile([P, P], BF16)
        make_identity(nc, ident_b[:])
        sel = const.tile([P, 2], BF16)
        nc.vector.tensor_tensor(out=sel[:], in0=ident_b[:, 14:16], in1=ident_b[:, 12:14], op=ALU.subtract)

        fcodes = const.tile([P, GC * B], U32, align_bytes=64)
        fscales = const.tile([P, GC * B], U8, align_bytes=64)
        hcodes = const.tile([P, GD * B], U32, align_bytes=64)
        hscales = const.tile([P, GD * B], U8, align_bytes=64)
        ncodes = const.tile([P, GD * B], U32, align_bytes=64)
        nscales = const.tile([P, GD * B], U8, align_bytes=64)
        bbias = const.tile([P, 3 * NP], BF16)
        dbias = const.tile([P, NP], F32)
        roi_sb = const.tile([P, NP, 4], BF16)

        def bbox_scale(g, c0, n):
            if g < 4:
                return bbox_pl[4 * g:P, c0:c0 + n]
            return mix_pl[8 + 4 * (g - 4):P, c0:c0 + n]

        def cls_scale(g, c0, n):
            if g < 4:
                return cls_pl[4 * g:P, c0:c0 + n]
            return mix_pl[4 * (g - 4):P, c0:c0 + n]

        def spread_bias(r, dst, on_vector, by_word=False):
            bp = psum.tile([P, BANK], F32, tag="bank", name="bp%d" % r)
            if r < 12:
                lhsT = ident_b[:, r:r + 1].to_broadcast([P, P])
            else:
                lhsT = sel[:, r - 12:r - 11].to_broadcast([P, P])
            nc.tensor.matmul(out=bp[:], lhsT=lhsT, rhs=brow[:], start=True, stop=True)
            src = bp[:].rearrange("p (q t) -> p t q", t=4) if by_word else bp[:]
            if on_vector:
                nc.vector.tensor_copy(out=dst, in_=src)
            else:
                nc.scalar.copy(out=dst, in_=src)

        with tc.tile_pool(name="s1", bufs=1) as s1:
            x_sb = s1.tile([P, C], BF16)
            nc.sync.dma_start(out=x_sb[:], in_=features.rearrange("b h w c -> b (h w c)"))
            conv_w = []

            def load_conv(g):
                w = wpool.tile([P, D], U32, tag="w12", bufs=8, name="convw%d" % g, align_bytes=64)
                nc.sync.dma_start(out=w[:].bitcast(I32), in_=words(conv_w_words[g]))
                conv_w.append(w)

            load_conv(0)
            for q in range(4):
                nc.gpsimd.dma_start(out=conv_pl[32 * q:32 * q + 16, :].bitcast(F32),
                                    in_=conv_w_scales[:, 4 * q:4 * q + 4, :].bitcast(F32))
            for g in range(1, GC):
                load_conv(g)
            nc.scalar.dma_start(out=brow[0:6, :], in_=conv_b.rearrange("(r c) -> r c", c=BANK))
            nc.scalar.dma_start(out=brow[6:12, :], in_=bbox_b[NP:4 * NP].rearrange("(r c) -> r c", c=BANK))
            nc.scalar.dma_start(out=brow[12:16, :], in_=cls_b.rearrange("(r c) -> r c", c=BANK))
            for q in range(4):
                nc.gpsimd.dma_start(out=bbox_pl[32 * q:32 * q + 16, :].bitcast(F32),
                                  in_=bbox_w_scales[0:4, 4 * q:4 * q + 4, NP:4 * NP].bitcast(F32))
            for q in range(4):
                nc.gpsimd.dma_start(out=mix_pl[32 * q + 8:32 * q + 16, :].bitcast(F32),
                                  in_=bbox_w_scales[4:6, 4 * q:4 * q + 4, NP:4 * NP].bitcast(F32))
            for q in range(4):
                nc.gpsimd.dma_start(out=mix_pl[32 * q:32 * q + 8, 0:2 * NP].bitcast(F32),
                                  in_=cls_w_scales[4:6, 4 * q:4 * q + 4, :].bitcast(F32))
            for q in range(4):
                nc.gpsimd.dma_start(out=cls_pl[32 * q:32 * q + 16, :].bitcast(F32),
                                  in_=cls_w_scales[0:4, 4 * q:4 * q + 4, :].bitcast(F32))
            b_w = []

            def load_b(g):
                w = wpool.tile([P, NB], U32, tag="w12", bufs=8, name="bw%d" % g, align_bytes=64)
                nc.sync.dma_start(out=w[:].bitcast(I32), in_=words(bbox_w_words[g][:, 4 * NP - NB:4 * NP, :]))
                b_w.append(w)

            for g in range(4):
                load_b(g)
            nc.sync.dma_start(out=roi_sb[:], in_=roi)

            x32 = x_sb[:].bitcast(F32)
            fgrouped = s1.tile([P, C], BF16, align_bytes=64)
            fg32 = fgrouped[:].bitcast(F32).rearrange("p (g b u) -> p g b u", g=GC, u=2)
            for a in range(GC // 2):
                xt = psum.tile([P, 2, 2, B], F32, tag="bank", name="xt%d" % a)
                for gg in range(2):
                    g = 2 * a + gg
                    for u in range(2):
                        nc.tensor.transpose(xt[:, gg, u, :], x32[:, 256 * g + u:256 * (g + 1):2], ident_f[:])
                nc.vector.tensor_copy(out=fg32[:, 2 * a:2 * a + 2, :, :], in_=xt[:].rearrange("p g u b -> p g b u"))
            nc.vector.quantize_mx(out=fcodes[:].bitcast(FP8X4), scales=fscales[:], in_=fgrouped[:])

            cbias = s1.tile([P, GD, 4, P], BF16)
            for r in range(6):
                spread_bias(r, cbias[:, r, :, :], r % 2 == 0, True)
            for r in range(6, 12):
                spread_bias(r, bbias[:, BANK * (r - 6):BANK * (r - 5)], r % 2 == 0)
            for r in range(12, 14):
                spread_bias(r, dbias[:, BANK * (r - 12):BANK * (r - 11)], r % 2 == 0)

            hacc = []
            for j in range(GD):
                acc = psum.tile([P, BANK], F32, tag="bank", name="hacc%d" % j)
                hacc.append(acc)
            for g in range(GC):
                for j in range(GD):
                    nc.tensor.matmul_mx(out=hacc[j][:],
                                        lhsT=fcodes[:, B * g:B * (g + 1)].bitcast(FP8X4),
                                        lhsT_scale=fscales[:, B * g:B * (g + 1)],
                                        rhs=conv_w[g][:, BANK * j:BANK * (j + 1)].bitcast(FP8X4),
                                        rhs_scale=conv_pl[4 * g:P, BANK * j:BANK * (j + 1)],
                                        start=(g == 0), stop=(g == GC - 1))
            for g in range(4, GD):
                load_b(g)
            hgs = []
            for j in range(GD):
                hperm = s1.tile([P, 4, P], BF16, tag="hperm", bufs=3, name="hperm%d" % j)
                nc.vector.tensor_tensor(out=hperm[:], in0=hacc[j][:].rearrange("p (q t) -> p t q", t=4),
                                        in1=cbias[:, j, :, :], op=ALU.add)
                ht = psum.tile([P, 4, B], BF16, tag="bank", name="ht%d" % j)
                for t in range(4):
                    nc.tensor.transpose(ht[:, t, :], hperm[:, t, :], ident_b[:])
                hg = s1.tile([P, B, 4], BF16, tag="hg", bufs=6, name="hg%d" % j, align_bytes=64)
                hgs.append(hg)
                nc.scalar.activation(out=hg[:], in_=ht[:].rearrange("p t b -> p b t"), func=ACT.Relu)
                nc.vector.quantize_mx(out=hcodes[:, B * j:B * (j + 1)].bitcast(FP8X4),
                                      scales=hscales[:, B * j:B * (j + 1)],
                                      in_=hg[:].rearrange("p b t -> p (b t)"))
            for j in range(GD):
                hgn = s1.tile([P, B, 4], BF16, tag="hgn", bufs=3, name="hgn%d" % j, align_bytes=64)
                nc.scalar.activation(out=hgn[:], in_=hgs[j][:], func=ACT.Copy, scale=-1.0)
                nc.vector.quantize_mx(out=ncodes[:, B * j:B * (j + 1)].bitcast(FP8X4),
                                      scales=nscales[:, B * j:B * (j + 1)],
                                      in_=hgn[:].rearrange("p b t -> p (b t)"))

        def head_pass(acc, g, rhs, rhs_scale, start, stop, negated=False):
            codes = ncodes if negated else hcodes
            scales = nscales if negated else hscales
            nc.tensor.matmul_mx(out=acc,
                                lhsT=codes[:, B * g:B * (g + 1)].bitcast(FP8X4),
                                lhsT_scale=scales[:, B * g:B * (g + 1)],
                                rhs=rhs.bitcast(FP8X4), rhs_scale=rhs_scale,
                                start=start, stop=stop)

        with tc.tile_pool(name="s2", bufs=1) as s2:
            planes = s2.tile([P, 5, NP], F32)
            nc.scalar.activation(out=planes[:, 1, :], in_=roi_sb[:, :, 1], func=ACT.Copy, scale=16.0)
            for hf in range(2):
                sl = slice(BANK * hf, BANK * (hf + 1))
                m = s2.tile([P, BANK], F32, tag="u", bufs=2, name="m%d" % hf)
                nc.vector.scalar_tensor_tensor(out=m[:], in0=bbias[:, sl], scalar=16.0, in1=roi_sb[:, sl, 3],
                                               op0=ALU.mult, op1=ALU.mult)
                nc.vector.scalar_tensor_tensor(out=planes[:, 0, sl], in0=roi_sb[:, sl, 0], scalar=16.0, in1=m[:],
                                               op0=ALU.mult, op1=ALU.subtract)

            bacc = []
            for k in range(5):
                acc = psum.tile([P, BANK], F32, tag="bank", name="bacc%d" % k)
                bacc.append(acc)
            for g in range(GD):
                for k in (0, 2, 4, 1, 3):
                    head_pass(bacc[k][:], g, b_w[g][:, BANK * k:BANK * (k + 1)],
                              bbox_scale(g, BANK * (k + 1), BANK), g == 0, g == GD - 1)

            cls_w = []
            for g in range(4):
                w = wpool.tile([P, 2 * NP], U32, tag="w12", bufs=8, name="clsw%d" % g, align_bytes=64)
                nc.sync.dma_start(out=w[:].bitcast(I32), in_=words(cls_w_words[g]))
                cls_w.append(w)
            cls_last = {}
            for hf in (1, 0):
                for s in range(2):
                    n0 = NP * s + BANK * hf
                    w = wpool.tile([P, 2, BANK], U32, tag="tail", bufs=8, name="clsl%d_%d" % (hf, s), align_bytes=64)
                    nc.sync.dma_start(out=w[:].bitcast(I32),
                                      in_=cls_w_words[4:6, :, n0:n0 + BANK, :]
                                      .rearrange("g p n t -> p g (n t)").bitcast(I32))
                    cls_last[hf, s] = w
            x_w = {}
            for c in (1, 0):
                for g0, g1 in ((0, 4), (4, 6)):
                    w = wpool.tile([P, g1 - g0, CH], U32, tag="tail", bufs=8, name="xw%d_%d" % (c, g0), align_bytes=64)
                    nc.sync.dma_start(out=w[:].bitcast(I32),
                                      in_=bbox_w_words[g0:g1, :, NP + CH * c:NP + CH * (c + 1), :]
                                      .rearrange("g p n t -> p g (n t)").bitcast(I32))
                    for g in range(g0, g1):
                        x_w[c, g] = w[:, g - g0, :]

            obs = []
            for c in range(4):
                ob = s2.tile([P, CH, 5], F32, tag="ob", bufs=4, name="ob%d" % c)
                obs.append(ob)

            def cols(c):
                return slice(CH * c, CH * (c + 1))

            def lay(copy, c, o0, o1, p0, p1):
                copy(out=obs[c][:, o0:o1, p0:p1],
                     in_=planes[:, p0:p1, CH * c + o0:CH * c + o1].rearrange("p c n -> p n c"))

            def x_out(acc, sl, n):
                tx = s2.tile([P, n], F32, tag="tx", bufs=2, name="tx%d" % sl.start)
                nc.vector.scalar_tensor_tensor(out=tx[:], in0=acc, scalar=16.0, in1=roi_sb[:, sl, 3],
                                               op0=ALU.mult, op1=ALU.mult)
                nc.vector.tensor_tensor(out=planes[:, 0, sl], in0=planes[:, 0, sl], in1=tx[:], op=ALU.subtract)

            x_out(bacc[0][:], slice(BANK, NP), BANK)
            e = None
            for j in (1, 3, 0, 2):
                comp = 2 + j // 2
                sl = slice(BANK * (j % 2), BANK * (j % 2 + 1))
                u = s2.tile([P, BANK], F32, tag="u", bufs=2, name="u%d" % j)
                nc.vector.tensor_tensor(out=u[:], in0=bacc[j + 1][:], in1=bbias[:, NP + BANK * j:NP + BANK * (j + 1)],
                                        op=ALU.add)
                nc.vector.tensor_scalar(out=u[:], in0=u[:], scalar1=10.0, scalar2=-10.0, op0=ALU.min, op1=ALU.max)
                e = s2.tile([P, BANK], F32, tag="e", bufs=2, name="e%d" % j)
                nc.scalar.activation(out=e[:], in_=u[:], func=ACT.Exp)
                nc.vector.scalar_tensor_tensor(out=planes[:, comp, sl], in0=e[:], scalar=16.0, in1=roi_sb[:, sl, comp],
                                               op0=ALU.mult, op1=ALU.mult)
            warm = s2.tile([P, 1], F32)
            nc.scalar.activation(out=warm[:], in_=e[:, 0:1], func=ACT.Sigmoid)

            dacc = []
            for hf in range(2):
                acc = psum.tile([P, BANK], F32, tag="bank", name="dacc%d" % hf)
                dacc.append(acc)
            for g in range(4):
                for hf in (1, 0):
                    head_pass(dacc[hf][:], g, cls_w[g][:, NP + BANK * hf:NP + BANK * (hf + 1)],
                              cls_scale(g, NP + BANK * hf, BANK), g == 0, False)
                for hf in (1, 0):
                    head_pass(dacc[hf][:], g, cls_w[g][:, BANK * hf:BANK * (hf + 1)],
                              cls_scale(g, BANK * hf, BANK), False, False, negated=True)

            def objectness(c, o0, o1):
                hf, off = divmod(CH * c, BANK)
                sl = slice(CH * c + o0, CH * c + o1)
                d = s2.tile([P, o1 - o0], F32, tag="d", bufs=4, name="d%d" % sl.start)
                nc.vector.tensor_tensor(out=d[:], in0=dacc[hf][:, off + o0:off + o1], in1=dbias[:, sl], op=ALU.add)
                dst = obs[c][:, :, 4] if c == 1 else planes[:, 4, sl]
                nc.scalar.activation(out=dst, in_=d[:], func=ACT.Sigmoid)

            def store_part(c, o0, o1):
                nc.sync.dma_start(out=out[:, CH * c + o0:CH * c + o1, :], in_=obs[c][:, o0:o1, :])

            for hf in (1, 0):
                for s in range(2):
                    for g in range(4, GD):
                        head_pass(dacc[hf][:], g, cls_last[hf, s][:, g - 4, :], cls_scale(g, NP * s + BANK * hf, BANK),
                                  False, s == 1 and g == GD - 1, negated=(s == 0))
                if hf == 1:
                    parts = ((2, 0, P), (2, P, CH), (3, 0, CH))
                    for part in parts:
                        objectness(*part)
                    for part in parts:
                        lay(nc.vector.tensor_copy, *part, 0, 5)
                        store_part(*part)
            lay(nc.scalar.copy, 1, 0, CH, 1, 4)

            for c in (1, 0):
                objectness(c, 0, CH)
            lay(nc.scalar.copy, 0, 0, P, 1, 5)
            for c in (1, 0):
                acc = psum.tile([P, CH], F32, tag="bank", name="xacc%d" % c)
                for g in range(GD):
                    head_pass(acc[:], g, x_w[c, g], bbox_scale(g, CH * c, CH), g == 0, g == GD - 1)
                halves = [slice(CH * c + o, CH * c + o + P) for o in range(0, CH, P)]
                txs = []
                for i in range(2):
                    tx = s2.tile([P, P], F32, tag="txh", bufs=4, name="txh%d_%d" % (c, i))
                    nc.vector.scalar_tensor_tensor(out=tx[:], in0=acc[:, P * i:P * (i + 1)], scalar=16.0,
                                                   in1=roi_sb[:, halves[i], 3], op0=ALU.mult, op1=ALU.mult)
                    txs.append(tx)
                for i in range(2):
                    nc.vector.tensor_tensor(out=planes[:, 0, halves[i]], in0=planes[:, 0, halves[i]], in1=txs[i][:],
                                            op=ALU.subtract)
                for o in range(0, CH, P):
                    lay(nc.vector.tensor_copy, c, o, o + P, 0, 5 if c == 0 and o == P else 1)
                    store_part(c, o, o + P)
